import numpy as np
import ml_dtypes


def mxq(x, axis, fmt="e4m3"):
    dtype, down = {"e4m3": (ml_dtypes.float8_e4m3fn, 7), "e5m2": (ml_dtypes.float8_e5m2, 14)}[fmt]
    v = np.moveaxis(np.asarray(x, np.float32).astype(ml_dtypes.bfloat16).astype(np.float64), axis, -1)
    blocks = v.reshape(v.shape[:-1] + (-1, 32))
    amax = np.abs(blocks).max(-1, keepdims=True)
    byte = np.maximum(np.where(amax > 0, np.frexp(amax)[1] - 1 + 127, 0) - down, 1)
    scale = np.exp2(byte - 127.0)
    codes = (blocks / scale).astype(np.float32).astype(dtype).astype(np.float64)
    return np.moveaxis((codes * scale).reshape(v.shape), -1, axis)


WIDE = False


def mx_kscale(k):
    if not WIDE:
        return np.ones(k)
    levels = np.array([10, -10, 5, -5, 0])
    a = np.random.permutation(np.resize(levels, k // 512 * 4)).reshape(k // 512, 4)
    idx = np.arange(k)
    return np.exp2(a[idx // 512, idx % 128 // 32])


BF16 = ml_dtypes.bfloat16


def bf(x):
    return np.asarray(x, np.float32).astype(BF16)


def f64(x):
    return np.asarray(x).astype(np.float64)


T, B, D, U, V, E = 4, 256, 512, 512, 512, 8
G = 2 * E
GS = (T + 1) * E


def softmax(v):
    e = np.exp(v - v.max(-1, keepdims=True))
    return e / e.sum(-1, keepdims=True)


def setup_inputs():
    rn = np.random.standard_normal
    s = mx_kscale(D)
    return {
        "x": bf(rn((B, D)) * s),
        "ews0": bf(rn((D, U, E)) / np.sqrt(D) / s[:, None, None]),
        "ebs0": bf(rn((U, E)) * 0.5),
        "ew0": bf(rn((T, D, U, E)) / np.sqrt(D) / s[None, :, None, None]),
        "eb0": bf(rn((T, U, E)) * 0.5),
        "gate_pre0": bf(rn((T, B, G))),
        "gb0": bf(rn((T, G)) * 0.5),
        "sgate_pre": bf(rn((B, GS))),
        "gbs": bf(rn((GS,)) * 0.5),
    }


def reference(x, ews0, ebs0, ew0, eb0, gate_pre0, gb0, sgate_pre, gbs):
    xq = mxq(f64(x), 1, "e4m3")
    es = np.maximum((xq @ mxq(f64(ews0).reshape(D, U * E), 0, "e4m3")).reshape(B, U, E) + f64(ebs0), 0.0)
    et = np.maximum((xq @ mxq(f64(ew0).reshape(T, D, U * E), 1, "e4m3")).reshape(T, B, U, E) + f64(eb0)[:, None], 0.0)
    g = softmax(f64(gate_pre0) + f64(gb0)[:, None])
    comb = np.concatenate([et, np.broadcast_to(es, et.shape)], axis=-1)
    task_out = (comb * g[:, :, None, :]).sum(-1)
    gs = softmax(f64(sgate_pre) + f64(gbs))
    all_exp = np.concatenate([np.moveaxis(et, 0, 2).reshape(B, U, T * E), es], axis=-1)
    share_out = (all_exp * gs[:, None, :]).sum(-1)
    return task_out, share_out

@@ -1,0 +1,279 @@
+from contextlib import ExitStack
+
+import concourse.mybir as mybir
+from concourse.masks import make_identity
+
+F32 = mybir.dt.float32
+BF16 = mybir.dt.bfloat16
+U32 = mybir.dt.uint32
+U8 = mybir.dt.uint8
+FP8X4 = mybir.dt.float8_e4m3fn_x4
+ALU = mybir.AluOpType
+ACT = mybir.ActivationFunctionType
+AXIS_X = mybir.AxisListType.X
+
+P = 128
+PACK = 4
+T, B, D, U, E = 4, 256, 512, 512, 8
+SETS = T + 1
+SHARE = T
+B_BLOCKS = B // P
+U_BLOCKS = U // P
+E_GROUP = 4
+GROUPS = E // E_GROUP
+UNITS_PER_SET = GROUPS * U_BLOCKS
+N_UNITS = SETS * UNITS_PER_SET
+N_EXPERTS = SETS * E
+CHUNK = P * E
+G_TASK = 2 * E
+G_SHARE = SETS * E
+SUMS_PER_UNIT = 5
+LEAD_UNITS = 2
+
+FLOPS = 2 * B * D * U * E * SETS
+
+assert D == P * PACK
+
+
+def tile_plelayer_pa_kernel(
+    tc, x, ews0, ebs0, ew0, eb0, gate_pre0, gb0, sgate_pre, gbs, out_0, out_1
+):
+    nc = tc.nc
+    with ExitStack() as ctx:
+        const = ctx.enter_context(tc.tile_pool(name="const", bufs=1))
+        raw_pool = ctx.enter_context(tc.tile_pool(name="raw", bufs=2 * U_BLOCKS))
+        grouped_pool = ctx.enter_context(tc.tile_pool(name="grouped", bufs=4))
+        codes_pool = ctx.enter_context(tc.tile_pool(name="codes", bufs=6))
+        h_pool = ctx.enter_context(tc.tile_pool(name="h", bufs=3))
+        psum_mx = ctx.enter_context(tc.psum_pool(name="psum_mx", bufs=4))
+        psum_t = ctx.enter_context(tc.psum_pool(name="psum_t", bufs=4))
+
+        x_sb = const.tile([P, B_BLOCKS, D], BF16)
+        nc.sync.dma_start(out=x_sb[:], in_=x.rearrange("(bb p) d -> p bb d", p=P))
+
+        bias_bf = const.tile([P, SETS, U_BLOCKS, E], BF16)
+        nc.scalar.dma_start(out=bias_bf[:, 0], in_=ebs0.rearrange("(ub p) e -> p ub e", p=P))
+        nc.scalar.dma_start(out=bias_bf[:, 1:SETS], in_=eb0.rearrange("t (ub p) e -> p t ub e", p=P))
+
+        pre_task = const.tile([P, B_BLOCKS, T, G_TASK], BF16)
+        for bb in range(B_BLOCKS):
+            nc.scalar.dma_start(
+                out=pre_task[:, bb],
+                in_=gate_pre0[:, bb * P : (bb + 1) * P, :].rearrange("t p g -> p t g"),
+            )
+        pre_share = const.tile([P, B_BLOCKS, G_SHARE], BF16)
+        nc.scalar.dma_start(out=pre_share[:], in_=sgate_pre.rearrange("(bb p) g -> p bb g", p=P))
+        gb_task = const.tile([P, T * G_TASK], BF16)
+        nc.scalar.dma_start(out=gb_task[:], in_=gb0.rearrange("t g -> (t g)").partition_broadcast(P))
+        gb_share = const.tile([P, G_SHARE], BF16)
+        nc.scalar.dma_start(out=gb_share[:], in_=gbs.partition_broadcast(P))
+
+        raw_tiles = {}
+        grouped_tiles = {}
+        code_tiles = {}
+
+        def unit_index(j):
+            s, rest = divmod(j, UNITS_PER_SET)
+            eg, ub = divmod(rest, U_BLOCKS)
+            return s, eg, ub
+
+        def load_chunk(s, ub):
+            w = ews0 if s == 0 else ew0[s - 1]
+            rows = w.rearrange("(p t) u e -> p t (u e)", t=PACK)
+            raw = raw_pool.tile([P, PACK, CHUNK], BF16, name="raw")
+            nc.sync.dma_start(out=raw[:], in_=rows[:, :, ub * CHUNK : (ub + 1) * CHUNK])
+            raw_tiles[(s, ub)] = raw
+
+        def regroup(j, engine_copy):
+            s, eg, ub = unit_index(j)
+            grouped = grouped_pool.tile([P, E_GROUP, P, PACK], BF16, name="grouped", align_bytes=64)
+            source = raw_tiles[(s, ub)][:].rearrange("p t (u e) -> p u t e", e=E)
+            engine_copy(
+                out=grouped[:].rearrange("p i u t -> p u t i"),
+                in_=source[:, :, :, eg * E_GROUP : (eg + 1) * E_GROUP],
+            )
+            grouped_tiles[j] = grouped
+            if eg == GROUPS - 1 and s + 2 < SETS:
+                load_chunk(s + 2, ub)
+
+        def quantise(j):
+            s, eg, ub = unit_index(j)
+            if ub == 0:
+                codes = codes_pool.tile([P, U_BLOCKS, E_GROUP * P], U32, name="codes", align_bytes=64)
+                scales = codes_pool.tile([P, U_BLOCKS, E_GROUP * P], U8, name="scales", align_bytes=64)
+                code_tiles[(s, eg)] = (codes, scales)
+            codes, scales = code_tiles[(s, eg)]
+            nc.vector.quantize_mx(
+                out=codes[:, ub, :].bitcast(FP8X4),
+                scales=scales[:, ub, :],
+                in_=grouped_tiles[j][:].rearrange("p i u t -> p (i u t)"),
+            )
+
+        for s in range(2):
+            for ub in range(U_BLOCKS):
+                load_chunk(s, ub)
+
+        ident = const.tile([P, P], F32)
+        make_identity(nc, ident[:])
+        x_words = x_sb[:].bitcast(F32).rearrange("p bb (w j) -> p bb j w", j=2)
+        x_t = psum_t.tile([P, 2, B], F32, tag="h_t")
+        for bb in range(B_BLOCKS):
+            for j in range(2):
+                nc.tensor.transpose(
+                    out=x_t[:, j, bb * P : (bb + 1) * P], in_=x_words[:, bb, j, :], identity=ident[:]
+                )
+        x_grouped = const.tile([P, B, PACK], BF16, align_bytes=64)
+        nc.vector.tensor_copy(out=x_grouped[:].bitcast(F32), in_=x_t[:].rearrange("p j b -> p b j"))
+        x_codes = const.tile([P, B], U32, align_bytes=64)
+        x_scales = const.tile([P, B], U8, align_bytes=64)
+        nc.vector.quantize_mx(
+            out=x_codes[:].bitcast(FP8X4),
+            scales=x_scales[:],
+            in_=x_grouped[:].rearrange("p b t -> p (b t)"),
+        )
+
+        bias_f = const.tile([P, SETS, U_BLOCKS, E], F32)
+        nc.vector.tensor_copy(out=bias_f[:], in_=bias_bf[:])
+
+        def softmax_rows(logits, rows, width, label):
+            wide = [P, rows, width]
+            top = const.tile([P, rows], F32, name="top_" + label)
+            nc.vector.tensor_reduce(out=top[:], in_=logits, axis=AXIS_X, op=ALU.max)
+            nc.vector.tensor_tensor(
+                out=logits, in0=logits, in1=top[:].unsqueeze(2).to_broadcast(wide), op=ALU.subtract
+            )
+            nc.scalar.activation(out=logits, in_=logits, func=ACT.Exp)
+            total = const.tile([P, rows], F32, name="total_" + label)
+            nc.vector.tensor_reduce(out=total[:], in_=logits, axis=AXIS_X, op=ALU.add)
+            inverse = const.tile([P, rows], F32, name="inverse_" + label)
+            nc.vector.reciprocal(out=inverse[:], in_=total[:])
+            nc.vector.tensor_tensor(
+                out=logits, in0=logits, in1=inverse[:].unsqueeze(2).to_broadcast(wide), op=ALU.mult
+            )
+
+        g_task = const.tile([P, B_BLOCKS, T * G_TASK], F32)
+        nc.vector.tensor_tensor(
+            out=g_task[:],
+            in0=pre_task[:].rearrange("p bb t g -> p bb (t g)"),
+            in1=gb_task[:].unsqueeze(1).to_broadcast([P, B_BLOCKS, T * G_TASK]),
+            op=ALU.add,
+        )
+        softmax_rows(g_task[:].rearrange("p bb (t g) -> p (bb t) g", g=G_TASK), B_BLOCKS * T, G_TASK, "task")
+        g_share = const.tile([P, B_BLOCKS, G_SHARE], F32)
+        nc.vector.tensor_tensor(
+            out=g_share[:],
+            in0=pre_share[:],
+            in1=gb_share[:].unsqueeze(1).to_broadcast([P, B_BLOCKS, G_SHARE]),
+            op=ALU.add,
+        )
+        softmax_rows(g_share[:], B_BLOCKS, G_SHARE, "share")
+
+        sums = {}
+        for o in range(SETS):
+            for bb in range(B_BLOCKS):
+                sums[(o, bb)] = const.tile([P, U], F32, name="sum_%d_%d" % (o, bb))
+        products = {}
+        hidden = {}
+        hidden_t = {}
+
+        def multiply(k):
+            s, e = divmod(k, E)
+            eg, i = divmod(e, E_GROUP)
+            codes, scales = code_tiles[(s, eg)]
+            cols = slice(i * P, (i + 1) * P)
+            products[k] = []
+            for half in range(U_BLOCKS // 2):
+                product = psum_mx.tile([P, 2, B], F32, name="product")
+                for j in range(2):
+                    ub = 2 * half + j
+                    nc.tensor.matmul_mx(
+                        out=product[:, j, :],
+                        lhsT=codes[:, ub, cols].bitcast(FP8X4),
+                        lhsT_scale=scales[:, ub, cols],
+                        rhs=x_codes[:].bitcast(FP8X4),
+                        rhs_scale=x_scales[:],
+                        start=True,
+                        stop=True,
+                    )
+                products[k].append(product)
+
+        def bias_relu(k):
+            s, e = divmod(k, E)
+            h = h_pool.tile([P, U_BLOCKS, B], F32, name="h")
+            for ub in range(U_BLOCKS):
+                nc.scalar.activation(
+                    out=h[:, ub, :],
+                    in_=products[k][ub // 2][:, ub % 2, :],
+                    func=ACT.Relu,
+                    bias=bias_f[:, s, ub, e : e + 1],
+                    scale=1.0,
+                )
+            hidden[k] = h
+
+        def transpose(k):
+            hidden_t[k] = []
+            for bb in range(B_BLOCKS):
+                h_t = psum_t.tile([P, U], F32, name="h_t")
+                for ub in range(U_BLOCKS):
+                    nc.tensor.transpose(
+                        out=h_t[:, ub * P : (ub + 1) * P],
+                        in_=hidden[k][:, ub, bb * P : (bb + 1) * P],
+                        identity=ident[:],
+                    )
+                hidden_t[k].append(h_t)
+
+        def weighted_sums(k):
+            s, e = divmod(k, E)
+            if s == 0:
+                uses = [(t, g_task, t * G_TASK + E + e) for t in range(T)]
+                uses.append((SHARE, g_share, T * E + e))
+            else:
+                uses = [(s - 1, g_task, (s - 1) * G_TASK + e), (SHARE, g_share, (s - 1) * E + e)]
+            for bb in range(B_BLOCKS):
+                for o, gates, col in uses:
+                    gate = gates[:, bb, col : col + 1]
+                    if k == 0:
+                        nc.vector.tensor_scalar_mul(out=sums[(o, bb)][:], in0=hidden_t[k][bb][:], scalar1=gate)
+                    else:
+                        nc.vector.scalar_tensor_tensor(
+                            out=sums[(o, bb)][:],
+                            in0=hidden_t[k][bb][:],
+                            scalar=gate,
+                            in1=sums[(o, bb)][:],
+                            op0=ALU.mult,
+                            op1=ALU.add,
+                        )
+            if s > 0 and e == E - 1:
+                for bb in range(B_BLOCKS):
+                    nc.sync.dma_start(out=out_0[s - 1, bb * P : (bb + 1) * P, :], in_=sums[(s - 1, bb)][:])
+            return B_BLOCKS * len(uses)
+
+        for ub in range(U_BLOCKS):
+            regroup(ub, nc.vector.tensor_copy)
+            regroup(U_BLOCKS + ub, nc.scalar.copy)
+            if ub > 0:
+                quantise(ub - 1)
+                quantise(U_BLOCKS + ub - 1)
+        quantise(U_BLOCKS - 1)
+        quantise(2 * U_BLOCKS - 1)
+
+        regrouped = UNITS_PER_SET
+        quantised = UNITS_PER_SET
+        sums_written = 0
+        for k in range(N_EXPERTS + 2):
+            if k < N_EXPERTS:
+                multiply(k)
+                bias_relu(k)
+            if 1 <= k <= N_EXPERTS:
+                transpose(k - 1)
+            if k >= 2:
+                sums_written += weighted_sums(k - 2)
+            while quantised < regrouped:
+                quantise(quantised)
+                quantised += 1
+            while regrouped < min(N_UNITS, UNITS_PER_SET + LEAD_UNITS + sums_written // SUMS_PER_UNIT):
+                regroup(regrouped, nc.scalar.copy)
+                regrouped += 1
+
+        for bb in range(B_BLOCKS):
+            nc.sync.dma_start(out=out_1[bb * P : (bb + 1) * P, :], in_=sums[(SHARE, bb)][:])

@@ -16,19 +16,24 @@ P = 128
 PACK = 4
 T, B, D, U, E = 4, 256, 512, 512, 8
 SETS = T + 1
-SHARE = T
 B_BLOCKS = B // P
 U_BLOCKS = U // P
 E_GROUP = 4
 GROUPS = E // E_GROUP
-UNITS_PER_SET = GROUPS * U_BLOCKS
-N_UNITS = SETS * UNITS_PER_SET
-N_EXPERTS = SETS * E
+UNIT_WORDS = E_GROUP * P
+UNIT_COLS = UNIT_WORDS * PACK
 CHUNK = P * E
 G_TASK = 2 * E
 G_SHARE = SETS * E
-SUMS_PER_UNIT = 5
-LEAD_UNITS = 2
+N_TASK_EXPERTS = T * E
+GB = 16
+N_GROUPS = B // GB
+O_SLOTS = P // GB
+QUAD = 4
+FINISH_EARLY = 22
+PER_STEP = 2
+V_EVERY = 6
+LATE = 2
 
 FLOPS = 2 * B * D * U * E * SETS
 
@@ -41,12 +46,14 @@ def tile_plelayer_pa_kernel(
     nc = tc.nc
     with ExitStack() as ctx:
         const = ctx.enter_context(tc.tile_pool(name="const", bufs=1))
-        raw_pool = ctx.enter_context(tc.tile_pool(name="raw", bufs=2 * U_BLOCKS))
-        grouped_pool = ctx.enter_context(tc.tile_pool(name="grouped", bufs=4))
-        codes_pool = ctx.enter_context(tc.tile_pool(name="codes", bufs=6))
+        raw_pool = ctx.enter_context(tc.tile_pool(name="raw", bufs=6))
+        unit_pool = ctx.enter_context(tc.tile_pool(name="unit", bufs=4))
+        codes_pool = ctx.enter_context(tc.tile_pool(name="codes", bufs=5))
         h_pool = ctx.enter_context(tc.tile_pool(name="h", bufs=3))
-        psum_mx = ctx.enter_context(tc.psum_pool(name="psum_mx", bufs=4))
-        psum_t = ctx.enter_context(tc.psum_pool(name="psum_t", bufs=4))
+        rows_pool = ctx.enter_context(tc.tile_pool(name="rows", bufs=3))
+        part_pool = ctx.enter_context(tc.tile_pool(name="part", bufs=2))
+        psum_mx = ctx.enter_context(tc.psum_pool(name="psum_mx", bufs=3))
+        psum_t = ctx.enter_context(tc.psum_pool(name="psum_t", bufs=5))
 
         x_sb = const.tile([P, B_BLOCKS, D], BF16)
         nc.sync.dma_start(out=x_sb[:], in_=x.rearrange("(bb p) d -> p bb d", p=P))
@@ -69,49 +76,49 @@ def tile_plelayer_pa_kernel(
         nc.scalar.dma_start(out=gb_share[:], in_=gbs.partition_broadcast(P))
 
         raw_tiles = {}
-        grouped_tiles = {}
         code_tiles = {}
+        unit_tiles = {}
+        loads = [(s, ub) for s in range(SETS) for ub in range(U_BLOCKS)]
+        loaded = {"count": 0}
 
-        def unit_index(j):
-            s, rest = divmod(j, UNITS_PER_SET)
-            eg, ub = divmod(rest, U_BLOCKS)
-            return s, eg, ub
+        def load_next():
+            if loaded["count"] < len(loads):
+                s, ub = loads[loaded["count"]]
+                loaded["count"] += 1
+                w = ews0 if s == 0 else ew0[s - 1]
+                rows = w.rearrange("(p t) u e -> p t (u e)", t=PACK)
+                raw = raw_pool.tile([P, PACK, CHUNK], BF16, name="raw")
+                nc.sync.dma_start(out=raw[:], in_=rows[:, :, ub * CHUNK : (ub + 1) * CHUNK])
+                raw_tiles[(s, ub)] = raw
 
-        def load_chunk(s, ub):
-            w = ews0 if s == 0 else ew0[s - 1]
-            rows = w.rearrange("(p t) u e -> p t (u e)", t=PACK)
-            raw = raw_pool.tile([P, PACK, CHUNK], BF16, name="raw")
-            nc.sync.dma_start(out=raw[:], in_=rows[:, :, ub * CHUNK : (ub + 1) * CHUNK])
-            raw_tiles[(s, ub)] = raw
-
-        def regroup(j, engine_copy):
-            s, eg, ub = unit_index(j)
-            grouped = grouped_pool.tile([P, E_GROUP, P, PACK], BF16, name="grouped", align_bytes=64)
+        def regroup(s, eg, ub, engine):
+            grouped = unit_pool.tile([P, E_GROUP, P, PACK], BF16, name="unit", align_bytes=64)
             source = raw_tiles[(s, ub)][:].rearrange("p t (u e) -> p u t e", e=E)
-            engine_copy(
-                out=grouped[:].rearrange("p i u t -> p u t i"),
-                in_=source[:, :, :, eg * E_GROUP : (eg + 1) * E_GROUP],
-            )
-            grouped_tiles[j] = grouped
-            if eg == GROUPS - 1 and s + 2 < SETS:
-                load_chunk(s + 2, ub)
+            source = source[:, :, :, eg * E_GROUP : (eg + 1) * E_GROUP]
+            target = grouped[:].rearrange("p i u t -> p u t i")
+            if engine == "V":
+                nc.vector.tensor_copy(out=target, in_=source)
+            else:
+                nc.scalar.copy(out=target, in_=source)
+            unit_tiles[(s, eg, ub)] = grouped
+            if eg == GROUPS - 1:
+                load_next()
 
-        def quantise(j):
-            s, eg, ub = unit_index(j)
-            if ub == 0:
-                codes = codes_pool.tile([P, U_BLOCKS, E_GROUP * P], U32, name="codes", align_bytes=64)
-                scales = codes_pool.tile([P, U_BLOCKS, E_GROUP * P], U8, name="scales", align_bytes=64)
+        def quantise(s, eg, ub):
+            if (s, eg) not in code_tiles:
+                codes = codes_pool.tile([P, U_BLOCKS * UNIT_WORDS], U32, name="codes", align_bytes=64)
+                scales = codes_pool.tile([P, U_BLOCKS * UNIT_WORDS], U8, name="scales", align_bytes=64)
                 code_tiles[(s, eg)] = (codes, scales)
             codes, scales = code_tiles[(s, eg)]
+            cols = slice(ub * UNIT_WORDS, (ub + 1) * UNIT_WORDS)
             nc.vector.quantize_mx(
-                out=codes[:, ub, :].bitcast(FP8X4),
-                scales=scales[:, ub, :],
-                in_=grouped_tiles[j][:].rearrange("p i u t -> p (i u t)"),
+                out=codes[:, cols].bitcast(FP8X4),
+                scales=scales[:, cols],
+                in_=unit_tiles[(s, eg, ub)][:].rearrange("p i u t -> p (i u t)"),
             )
 
-        for s in range(2):
-            for ub in range(U_BLOCKS):
-                load_chunk(s, ub)
+        for first in range(6):
+            load_next()
 
         ident = const.tile([P, P], F32)
         make_identity(nc, ident[:])
@@ -168,112 +175,225 @@ def tile_plelayer_pa_kernel(
         )
         softmax_rows(g_share[:], B_BLOCKS, G_SHARE, "share")
 
-        sums = {}
+        gates_s = const.tile([P, B_BLOCKS, SETS, E], F32)
+        nc.vector.tensor_copy(
+            out=gates_s[:, :, 0:T, :],
+            in_=g_task[:].rearrange("p bb (t g) -> p bb t g", g=G_TASK)[:, :, :, E:G_TASK],
+        )
+        nc.vector.tensor_copy(out=gates_s[:, :, T, :], in_=g_share[:, :, T * E : G_SHARE])
+        own_row = const.tile([P, GB], F32)
+        nc.vector.tensor_reduce(
+            out=own_row[:], in_=ident[:].rearrange("p (g c) -> p c g", c=GB), axis=AXIS_X, op=ALU.add
+        )
+        spread = const.tile([P, B_BLOCKS, SETS * E, GB], F32)
+        for bb in range(B_BLOCKS):
+            nc.vector.tensor_tensor(
+                out=spread[:, bb],
+                in0=gates_s[:, bb].rearrange("p o e -> p (o e)").unsqueeze(2).to_broadcast([P, SETS * E, GB]),
+                in1=own_row[:].unsqueeze(1).to_broadcast([P, SETS * E, GB]),
+                op=ALU.mult,
+            )
+        mixer = const.tile([P, N_GROUPS, O_SLOTS, GB], F32)
+        nc.gpsimd.memset(mixer[:], 0.0)
+        per_block = N_GROUPS // B_BLOCKS
+        for bb in range(B_BLOCKS):
+            turned = psum_t.tile([P, T, P], F32, name="h_t")
+            for o in range(T):
+                nc.tensor.transpose(
+                    out=turned[:, o, :],
+                    in_=spread[:, bb, o * E : (o + 1) * E, :].rearrange("p e c -> p (e c)"),
+                    identity=ident[:],
+                )
+            nc.vector.tensor_copy(
+                out=mixer[:, bb * per_block : (bb + 1) * per_block, 0:T, :],
+                in_=turned[:].rearrange("p o (g c) -> p g o c", c=GB),
+            )
+        turned = psum_t.tile([P, B_BLOCKS, P], F32, name="h_t")
+        for bb in range(B_BLOCKS):
+            nc.tensor.transpose(
+                out=turned[:, bb, :],
+                in_=spread[:, bb, T * E : SETS * E, :].rearrange("p e c -> p (e c)"),
+                identity=ident[:],
+            )
+        nc.vector.tensor_copy(
+            out=mixer[:, :, T, :], in_=turned[:].rearrange("p bb (g c) -> p (bb g) c", c=GB)
+        )
+
+        sums = [const.tile([P, B_BLOCKS, U], F32, name="sum_%d" % o) for o in range(SETS)]
+        early = [o for o in range(SETS) if o < LATE or o == T]
+        shared_part = {}
+        for o in early:
+            shared_part[o] = const.tile([P, B_BLOCKS, U], F32, name="shared_part_%d" % o)
+        terms = {}
         for o in range(SETS):
-            for bb in range(B_BLOCKS):
-                sums[(o, bb)] = const.tile([P, U], F32, name="sum_%d_%d" % (o, bb))
+            terms[o] = 0 if o in early else 1
+        hidden_s = [const.tile([P, N_GROUPS, E, GB], F32, name="hidden_s_%d" % ub) for ub in range(U_BLOCKS)]
         products = {}
         hidden = {}
         hidden_t = {}
 
-        def multiply(k):
-            s, e = divmod(k, E)
+        def multiply(s, e):
             eg, i = divmod(e, E_GROUP)
             codes, scales = code_tiles[(s, eg)]
-            cols = slice(i * P, (i + 1) * P)
-            products[k] = []
+            products[(s, e)] = []
             for half in range(U_BLOCKS // 2):
                 product = psum_mx.tile([P, 2, B], F32, name="product")
                 for j in range(2):
                     ub = 2 * half + j
+                    cols = slice(ub * UNIT_WORDS + i * P, ub * UNIT_WORDS + (i + 1) * P)
                     nc.tensor.matmul_mx(
                         out=product[:, j, :],
-                        lhsT=codes[:, ub, cols].bitcast(FP8X4),
-                        lhsT_scale=scales[:, ub, cols],
+                        lhsT=codes[:, cols].bitcast(FP8X4),
+                        lhsT_scale=scales[:, cols],
                         rhs=x_codes[:].bitcast(FP8X4),
                         rhs_scale=x_scales[:],
                         start=True,
                         stop=True,
                     )
-                products[k].append(product)
+                products[(s, e)].append(product)
 
-        def bias_relu(k):
-            s, e = divmod(k, E)
-            h = h_pool.tile([P, U_BLOCKS, B], F32, name="h")
+        def bias_relu(s, e):
+            if s > 0:
+                hidden[(s, e)] = h_pool.tile([P, U_BLOCKS, B], F32, name="h")
             for ub in range(U_BLOCKS):
+                source = products[(s, e)][ub // 2][:, ub % 2, :]
+                if s == 0:
+                    target = hidden_s[ub][:, :, e, :]
+                    source = source.rearrange("p (g c) -> p g c", c=GB)
+                else:
+                    target = hidden[(s, e)][:, ub, :]
                 nc.scalar.activation(
-                    out=h[:, ub, :],
-                    in_=products[k][ub // 2][:, ub % 2, :],
-                    func=ACT.Relu,
-                    bias=bias_f[:, s, ub, e : e + 1],
-                    scale=1.0,
+                    out=target, in_=source, func=ACT.Relu, bias=bias_f[:, s, ub, e : e + 1], scale=1.0
                 )
-            hidden[k] = h
 
-        def transpose(k):
-            hidden_t[k] = []
+        def transpose(s, e):
+            hidden_t[(s, e)] = []
             for bb in range(B_BLOCKS):
                 h_t = psum_t.tile([P, U], F32, name="h_t")
                 for ub in range(U_BLOCKS):
                     nc.tensor.transpose(
                         out=h_t[:, ub * P : (ub + 1) * P],
-                        in_=hidden[k][:, ub, bb * P : (bb + 1) * P],
+                        in_=hidden[(s, e)][:, ub, bb * P : (bb + 1) * P],
                         identity=ident[:],
                     )
-                hidden_t[k].append(h_t)
+                hidden_t[(s, e)].append(h_t)
 
-        def weighted_sums(k):
-            s, e = divmod(k, E)
-            if s == 0:
-                uses = [(t, g_task, t * G_TASK + E + e) for t in range(T)]
-                uses.append((SHARE, g_share, T * E + e))
-            else:
-                uses = [(s - 1, g_task, (s - 1) * G_TASK + e), (SHARE, g_share, (s - 1) * E + e)]
+        def finish(o):
+            for bb in range(B_BLOCKS):
+                if o in early:
+                    nc.vector.tensor_tensor(
+                        out=sums[o][:, bb, :], in0=sums[o][:, bb, :], in1=shared_part[o][:, bb, :], op=ALU.add
+                    )
+                target = out_0[o] if o < T else out_1
+                nc.sync.dma_start(out=target[bb * P : (bb + 1) * P, :], in_=sums[o][:, bb, :])
+
+        def weighted_sums(s, e):
+            uses = [(s - 1, g_task, (s - 1) * G_TASK + e), (T, g_share, (s - 1) * E + e)]
             for bb in range(B_BLOCKS):
                 for o, gates, col in uses:
                     gate = gates[:, bb, col : col + 1]
-                    if k == 0:
-                        nc.vector.tensor_scalar_mul(out=sums[(o, bb)][:], in0=hidden_t[k][bb][:], scalar1=gate)
+                    if terms[o] == 0:
+                        nc.vector.tensor_scalar_mul(out=sums[o][:, bb, :], in0=hidden_t[(s, e)][bb][:], scalar1=gate)
                     else:
                         nc.vector.scalar_tensor_tensor(
-                            out=sums[(o, bb)][:],
-                            in0=hidden_t[k][bb][:],
+                            out=sums[o][:, bb, :],
+                            in0=hidden_t[(s, e)][bb][:],
                             scalar=gate,
-                            in1=sums[(o, bb)][:],
+                            in1=sums[o][:, bb, :],
                             op0=ALU.mult,
                             op1=ALU.add,
                         )
-            if s > 0 and e == E - 1:
-                for bb in range(B_BLOCKS):
-                    nc.sync.dma_start(out=out_0[s - 1, bb * P : (bb + 1) * P, :], in_=sums[(s - 1, bb)][:])
-            return B_BLOCKS * len(uses)
+            for o, gates, col in uses:
+                terms[o] += 1
+
+        group_rows = {}
+        group_parts = {}
+        part_tiles = {}
+
+        def group_turn(g):
+            turned_g = psum_t.tile([P, U], F32, name="h_t")
+            for ub in range(U_BLOCKS):
+                nc.tensor.transpose(
+                    out=turned_g[:, ub * P : (ub + 1) * P],
+                    in_=hidden_s[ub][:, g].rearrange("p e c -> p (e c)"),
+                    identity=ident[:],
+                )
+            rows = rows_pool.tile([P, U], F32, name="rows")
+            nc.scalar.copy(out=rows[:], in_=turned_g[:])
+            group_rows[g] = rows
+
+        def group_mix(g):
+            mixed = psum_t.tile([P, U], F32, name="h_t")
+            nc.tensor.matmul(
+                out=mixed[:],
+                lhsT=mixer[:, g].rearrange("p o c -> p (o c)"),
+                rhs=group_rows[g][:],
+                start=True,
+                stop=True,
+            )
+            group_parts[g] = mixed
+
+        def group_out(g):
+            quad, place = divmod(g, QUAD)
+            if place == 0:
+                part_tiles[quad] = part_pool.tile([P, QUAD, U], F32, name="part")
+            nc.scalar.copy(out=part_tiles[quad][:, place, :], in_=group_parts[g][:])
+            if place == QUAD - 1:
+                rows = slice(quad * QUAD * GB, (quad + 1) * QUAD * GB)
+                for o in range(SETS):
+                    target = out_0[o] if o < T else out_1
+                    nc.gpsimd.dma_start(
+                        out=target[rows, :].rearrange("(q c) u -> c q u", c=GB),
+                        in_=part_tiles[quad][o * GB : (o + 1) * GB, :, :],
+                    )
+            if g == N_GROUPS - 1:
+                for o in range(SETS):
+                    source = out_0[o] if o < T else out_1
+                    target = shared_part[o] if o in early else sums[o]
+                    nc.gpsimd.dma_start(out=target[:], in_=source.rearrange("(bb p) u -> p bb u", p=P))
 
         for ub in range(U_BLOCKS):
-            regroup(ub, nc.vector.tensor_copy)
-            regroup(U_BLOCKS + ub, nc.scalar.copy)
+            regroup(0, 0, ub, "V")
+            regroup(0, 1, ub, "S")
             if ub > 0:
-                quantise(ub - 1)
-                quantise(U_BLOCKS + ub - 1)
-        quantise(U_BLOCKS - 1)
-        quantise(2 * U_BLOCKS - 1)
+                quantise(0, 0, ub - 1)
+                quantise(0, 1, ub - 1)
+        quantise(0, 0, U_BLOCKS - 1)
+        quantise(0, 1, U_BLOCKS - 1)
+        set_1 = [(1, eg, ub) for eg in range(GROUPS) for ub in range(U_BLOCKS)]
+        for e in range(E):
+            multiply(0, e)
+            bias_relu(0, e)
+            regroup(*set_1[e], "V")
+            if e > 0:
+                quantise(*set_1[e - 1])
+        quantise(*set_1[E - 1])
 
-        regrouped = UNITS_PER_SET
-        quantised = UNITS_PER_SET
-        sums_written = 0
-        for k in range(N_EXPERTS + 2):
-            if k < N_EXPERTS:
-                multiply(k)
-                bias_relu(k)
-            if 1 <= k <= N_EXPERTS:
-                transpose(k - 1)
-            if k >= 2:
-                sums_written += weighted_sums(k - 2)
-            while quantised < regrouped:
-                quantise(quantised)
-                quantised += 1
-            while regrouped < min(N_UNITS, UNITS_PER_SET + LEAD_UNITS + sums_written // SUMS_PER_UNIT):
-                regroup(regrouped, nc.scalar.copy)
-                regrouped += 1
-
-        for bb in range(B_BLOCKS):
-            nc.sync.dma_start(out=out_1[bb * P : (bb + 1) * P, :], in_=sums[(SHARE, bb)][:])
+        later = [(s, eg, ub) for s in range(2, SETS) for eg in range(GROUPS) for ub in range(U_BLOCKS)]
+        experts = [(1 + t, e) for t in range(T) for e in range(E)]
+        for i in range(N_TASK_EXPERTS + 2):
+            if i < N_TASK_EXPERTS:
+                multiply(*experts[i])
+                bias_relu(*experts[i])
+            if 1 <= i <= N_TASK_EXPERTS:
+                transpose(*experts[i - 1])
+            for g in range(PER_STEP * i, PER_STEP * (i + 1)):
+                if g < N_GROUPS:
+                    group_turn(g)
+                if 0 <= g - PER_STEP < N_GROUPS:
+                    group_mix(g - PER_STEP)
+                if 0 <= g - 2 * PER_STEP < N_GROUPS:
+                    group_out(g - 2 * PER_STEP)
+            if i >= 2:
+                weighted_sums(*experts[i - 2])
+                s, e = experts[i - 2]
+                if e == E - 1 and s - 1 >= LATE:
+                    finish(s - 1)
+                if i - 2 == FINISH_EARLY:
+                    for o in range(LATE):
+                        finish(o)
+            if 3 <= i < 3 + len(later):
+                quantise(*later[i - 3])
+            if 1 <= i < 1 + len(later):
+                regroup(*later[i - 1], "V" if i % V_EVERY == 0 else "S")
+        finish(T)

@@ -30,10 +30,23 @@ GB = 16
 N_GROUPS = B // GB
 O_SLOTS = P // GB
 QUAD = 4
-FINISH_EARLY = 22
-PER_STEP = 2
-V_EVERY = 6
-LATE = 2
+DIRECT = 2
+ADD_LAG = 3
+GROUP_FIRST = 1
+UNIT_LEAD = 5
+S_UNITS_FROM = 100
+S_UNITS_EVERY = 3
+ROWS_V = 100
+PART_V = 100
+FINISH_AT = 20
+MANUAL = 1
+AHEAD_EVERY = 8
+PIECES = 4
+PIECES_A_STEP = 2
+S_FIRST = 1
+DIRECT_EVERY = 1000
+Z_BUFS = 3
+HT_BUFS = 3
 
 FLOPS = 2 * B * D * U * E * SETS
 
@@ -45,15 +58,19 @@ def tile_plelayer_pa_kernel(
 ):
     nc = tc.nc
     with ExitStack() as ctx:
+        if MANUAL:
+            ctx.enter_context(tc.manual_schedule())
         const = ctx.enter_context(tc.tile_pool(name="const", bufs=1))
         raw_pool = ctx.enter_context(tc.tile_pool(name="raw", bufs=6))
         unit_pool = ctx.enter_context(tc.tile_pool(name="unit", bufs=4))
         codes_pool = ctx.enter_context(tc.tile_pool(name="codes", bufs=5))
         h_pool = ctx.enter_context(tc.tile_pool(name="h", bufs=3))
-        rows_pool = ctx.enter_context(tc.tile_pool(name="rows", bufs=3))
+        rows_pool = ctx.enter_context(tc.tile_pool(name="rows", bufs=2))
         part_pool = ctx.enter_context(tc.tile_pool(name="part", bufs=2))
-        psum_mx = ctx.enter_context(tc.psum_pool(name="psum_mx", bufs=3))
-        psum_t = ctx.enter_context(tc.psum_pool(name="psum_t", bufs=5))
+        gated_pool = ctx.enter_context(tc.tile_pool(name="gated", bufs=4))
+        psum_mx = ctx.enter_context(tc.psum_pool(name="psum_mx", bufs=Z_BUFS))
+        psum_t = ctx.enter_context(tc.psum_pool(name="psum_t", bufs=HT_BUFS))
+        psum_acc = ctx.enter_context(tc.psum_pool(name="psum_acc", bufs=1))
 
         x_sb = const.tile([P, B_BLOCKS, D], BF16)
         nc.sync.dma_start(out=x_sb[:], in_=x.rearrange("(bb p) d -> p bb d", p=P))
@@ -80,6 +97,7 @@ def tile_plelayer_pa_kernel(
         unit_tiles = {}
         loads = [(s, ub) for s in range(SETS) for ub in range(U_BLOCKS)]
         loaded = {"count": 0}
+        readers = {}
 
         def load_next():
             if loaded["count"] < len(loads):
@@ -91,18 +109,22 @@ def tile_plelayer_pa_kernel(
                 nc.sync.dma_start(out=raw[:], in_=rows[:, :, ub * CHUNK : (ub + 1) * CHUNK])
                 raw_tiles[(s, ub)] = raw
 
-        def regroup(s, eg, ub, engine):
-            grouped = unit_pool.tile([P, E_GROUP, P, PACK], BF16, name="unit", align_bytes=64)
+        def regroup(s, eg, ub, engine, piece=0, pieces=1):
+            if piece == 0:
+                unit_tiles[(s, eg, ub)] = unit_pool.tile([P, E_GROUP, P, PACK], BF16, name="unit", align_bytes=64)
+            grouped = unit_tiles[(s, eg, ub)]
+            span = slice(piece * (P // pieces), (piece + 1) * (P // pieces))
             source = raw_tiles[(s, ub)][:].rearrange("p t (u e) -> p u t e", e=E)
-            source = source[:, :, :, eg * E_GROUP : (eg + 1) * E_GROUP]
-            target = grouped[:].rearrange("p i u t -> p u t i")
+            source = source[:, span, :, eg * E_GROUP : (eg + 1) * E_GROUP]
+            target = grouped[:].rearrange("p i u t -> p u t i")[:, span]
             if engine == "V":
                 nc.vector.tensor_copy(out=target, in_=source)
             else:
                 nc.scalar.copy(out=target, in_=source)
-            unit_tiles[(s, eg, ub)] = grouped
-            if eg == GROUPS - 1:
-                load_next()
+            if piece == pieces - 1:
+                readers[(s, ub)] = readers.get((s, ub), 0) + 1
+                if readers[(s, ub)] == GROUPS:
+                    load_next()
 
         def quantise(s, eg, ub):
             if (s, eg) not in code_tiles:
@@ -138,11 +160,13 @@ def tile_plelayer_pa_kernel(
             scales=x_scales[:],
             in_=x_grouped[:].rearrange("p b t -> p (b t)"),
         )
-
         bias_f = const.tile([P, SETS, U_BLOCKS, E], F32)
         nc.vector.tensor_copy(out=bias_f[:], in_=bias_bf[:])
 
-        def softmax_rows(logits, rows, width, label):
+        g_task = const.tile([P, B_BLOCKS, T * G_TASK], F32)
+        g_share = const.tile([P, B_BLOCKS, G_SHARE], F32)
+
+        def softmax_head(logits, rows, width, label):
             wide = [P, rows, width]
             top = const.tile([P, rows], F32, name="top_" + label)
             nc.vector.tensor_reduce(out=top[:], in_=logits, axis=AXIS_X, op=ALU.max)
@@ -150,6 +174,9 @@ def tile_plelayer_pa_kernel(
                 out=logits, in0=logits, in1=top[:].unsqueeze(2).to_broadcast(wide), op=ALU.subtract
             )
             nc.scalar.activation(out=logits, in_=logits, func=ACT.Exp)
+
+        def softmax_tail(logits, rows, width, label):
+            wide = [P, rows, width]
             total = const.tile([P, rows], F32, name="total_" + label)
             nc.vector.tensor_reduce(out=total[:], in_=logits, axis=AXIS_X, op=ALU.add)
             inverse = const.tile([P, rows], F32, name="inverse_" + label)
@@ -158,79 +185,90 @@ def tile_plelayer_pa_kernel(
                 out=logits, in0=logits, in1=inverse[:].unsqueeze(2).to_broadcast(wide), op=ALU.mult
             )
 
-        g_task = const.tile([P, B_BLOCKS, T * G_TASK], F32)
+        task_rows = g_task[:].rearrange("p bb (t g) -> p (bb t) g", g=G_TASK)
         nc.vector.tensor_tensor(
             out=g_task[:],
             in0=pre_task[:].rearrange("p bb t g -> p bb (t g)"),
             in1=gb_task[:].unsqueeze(1).to_broadcast([P, B_BLOCKS, T * G_TASK]),
             op=ALU.add,
         )
-        softmax_rows(g_task[:].rearrange("p bb (t g) -> p (bb t) g", g=G_TASK), B_BLOCKS * T, G_TASK, "task")
-        g_share = const.tile([P, B_BLOCKS, G_SHARE], F32)
+        softmax_head(task_rows, B_BLOCKS * T, G_TASK, "task")
         nc.vector.tensor_tensor(
             out=g_share[:],
             in0=pre_share[:],
             in1=gb_share[:].unsqueeze(1).to_broadcast([P, B_BLOCKS, G_SHARE]),
             op=ALU.add,
         )
-        softmax_rows(g_share[:], B_BLOCKS, G_SHARE, "share")
+        softmax_head(g_share[:], B_BLOCKS, G_SHARE, "share")
+        softmax_tail(task_rows, B_BLOCKS * T, G_TASK, "task")
+        softmax_tail(g_share[:], B_BLOCKS, G_SHARE, "share")
 
-        gates_s = const.tile([P, B_BLOCKS, SETS, E], F32)
-        nc.vector.tensor_copy(
-            out=gates_s[:, :, 0:T, :],
-            in_=g_task[:].rearrange("p bb (t g) -> p bb t g", g=G_TASK)[:, :, :, E:G_TASK],
-        )
-        nc.vector.tensor_copy(out=gates_s[:, :, T, :], in_=g_share[:, :, T * E : G_SHARE])
-        own_row = const.tile([P, GB], F32)
-        nc.vector.tensor_reduce(
-            out=own_row[:], in_=ident[:].rearrange("p (g c) -> p c g", c=GB), axis=AXIS_X, op=ALU.add
-        )
-        spread = const.tile([P, B_BLOCKS, SETS * E, GB], F32)
-        for bb in range(B_BLOCKS):
-            nc.vector.tensor_tensor(
-                out=spread[:, bb],
-                in0=gates_s[:, bb].rearrange("p o e -> p (o e)").unsqueeze(2).to_broadcast([P, SETS * E, GB]),
-                in1=own_row[:].unsqueeze(1).to_broadcast([P, SETS * E, GB]),
-                op=ALU.mult,
-            )
         mixer = const.tile([P, N_GROUPS, O_SLOTS, GB], F32)
         nc.gpsimd.memset(mixer[:], 0.0)
-        per_block = N_GROUPS // B_BLOCKS
-        for bb in range(B_BLOCKS):
-            turned = psum_t.tile([P, T, P], F32, name="h_t")
-            for o in range(T):
+
+        def make_mixer():
+            gates_s = const.tile([P, B_BLOCKS, SETS, E], F32)
+            nc.vector.tensor_copy(
+                out=gates_s[:, :, 0:T, :],
+                in_=g_task[:].rearrange("p bb (t g) -> p bb t g", g=G_TASK)[:, :, :, E:G_TASK],
+            )
+            nc.vector.tensor_copy(out=gates_s[:, :, T, :], in_=g_share[:, :, T * E : G_SHARE])
+            own_row = const.tile([P, GB], F32)
+            nc.vector.tensor_reduce(
+                out=own_row[:], in_=ident[:].rearrange("p (g c) -> p c g", c=GB), axis=AXIS_X, op=ALU.add
+            )
+            spread = const.tile([P, B_BLOCKS, SETS * E, GB], F32)
+            for bb in range(B_BLOCKS):
+                nc.vector.tensor_tensor(
+                    out=spread[:, bb],
+                    in0=gates_s[:, bb].rearrange("p o e -> p (o e)").unsqueeze(2).to_broadcast([P, SETS * E, GB]),
+                    in1=own_row[:].unsqueeze(1).to_broadcast([P, SETS * E, GB]),
+                    op=ALU.mult,
+                )
+            per_block = N_GROUPS // B_BLOCKS
+            for bb in range(B_BLOCKS):
+                turned = psum_t.tile([P, T, P], F32, name="h_t")
+                for o in range(T):
+                    nc.tensor.transpose(
+                        out=turned[:, o, :],
+                        in_=spread[:, bb, o * E : (o + 1) * E, :].rearrange("p e c -> p (e c)"),
+                        identity=ident[:],
+                    )
+                nc.scalar.copy(
+                    out=mixer[:, bb * per_block : (bb + 1) * per_block, 0:T, :],
+                    in_=turned[:].rearrange("p o (g c) -> p g o c", c=GB),
+                )
+            turned = psum_t.tile([P, B_BLOCKS, P], F32, name="h_t")
+            for bb in range(B_BLOCKS):
                 nc.tensor.transpose(
-                    out=turned[:, o, :],
-                    in_=spread[:, bb, o * E : (o + 1) * E, :].rearrange("p e c -> p (e c)"),
+                    out=turned[:, bb, :],
+                    in_=spread[:, bb, T * E : SETS * E, :].rearrange("p e c -> p (e c)"),
                     identity=ident[:],
                 )
-            nc.vector.tensor_copy(
-                out=mixer[:, bb * per_block : (bb + 1) * per_block, 0:T, :],
-                in_=turned[:].rearrange("p o (g c) -> p g o c", c=GB),
-            )
-        turned = psum_t.tile([P, B_BLOCKS, P], F32, name="h_t")
-        for bb in range(B_BLOCKS):
-            nc.tensor.transpose(
-                out=turned[:, bb, :],
-                in_=spread[:, bb, T * E : SETS * E, :].rearrange("p e c -> p (e c)"),
-                identity=ident[:],
-            )
-        nc.vector.tensor_copy(
-            out=mixer[:, :, T, :], in_=turned[:].rearrange("p bb (g c) -> p (bb g) c", c=GB)
-        )
+            nc.scalar.copy(out=mixer[:, :, T, :], in_=turned[:].rearrange("p bb (g c) -> p (bb g) c", c=GB))
 
+        experts = [(1 + t, e) for t in range(T) for e in range(E)]
         sums = [const.tile([P, B_BLOCKS, U], F32, name="sum_%d" % o) for o in range(SETS)]
-        early = [o for o in range(SETS) if o < LATE or o == T]
         shared_part = {}
-        for o in early:
+        for o in (0, T):
             shared_part[o] = const.tile([P, B_BLOCKS, U], F32, name="shared_part_%d" % o)
         terms = {}
-        for o in range(SETS):
-            terms[o] = 0 if o in early else 1
-        hidden_s = [const.tile([P, N_GROUPS, E, GB], F32, name="hidden_s_%d" % ub) for ub in range(U_BLOCKS)]
+        for o in range(1, T):
+            for bb in range(B_BLOCKS):
+                terms[(o, bb)] = 1
+        hidden_s = []
+        for ub in range(U_BLOCKS):
+            block = gated_pool.tile([P, N_GROUPS, E, GB], F32, name="gated")
+            hidden_s.append(block)
         products = {}
         hidden = {}
         hidden_t = {}
+        acc = [psum_acc.tile([P, U], F32, name="acc_%d" % half) for half in range(2)]
+        gated_tiles = {}
+        last_gated = N_TASK_EXPERTS - DIRECT - 1
+
+        def is_direct(n):
+            return n > last_gated or n % DIRECT_EVERY == DIRECT_EVERY - 1
 
         def multiply(s, e):
             eg, i = divmod(e, E_GROUP)
@@ -266,45 +304,86 @@ def tile_plelayer_pa_kernel(
                     out=target, in_=source, func=ACT.Relu, bias=bias_f[:, s, ub, e : e + 1], scale=1.0
                 )
 
-        def transpose(s, e):
-            hidden_t[(s, e)] = []
+        def transpose(n, bb):
+            s, e = experts[n]
+            h_t = psum_t.tile([P, U], F32, name="h_t")
+            for ub in range(U_BLOCKS):
+                nc.tensor.transpose(
+                    out=h_t[:, ub * P : (ub + 1) * P],
+                    in_=hidden[(s, e)][:, ub, bb * P : (bb + 1) * P],
+                    identity=ident[:],
+                )
+            hidden_t[(n, bb)] = h_t
+
+        def add_term(o, bb, source, gate):
+            if terms.get((o, bb), 0) == 0:
+                nc.vector.tensor_scalar_mul(out=sums[o][:, bb, :], in0=source, scalar1=gate)
+            else:
+                nc.vector.scalar_tensor_tensor(
+                    out=sums[o][:, bb, :], in0=source, scalar=gate, in1=sums[o][:, bb, :], op0=ALU.mult, op1=ALU.add
+                )
+            terms[(o, bb)] = terms.get((o, bb), 0) + 1
+
+        def on_vector(n, bb):
+            s, e = experts[n]
+            col = (s - 1) * G_TASK + e
+            add_term(s - 1, bb, hidden_t[(n, bb)][:], g_task[:, bb, col : col + 1])
+            if is_direct(n):
+                col = (s - 1) * E + e
+                add_term(T, bb, hidden_t[(n, bb)][:], g_share[:, bb, col : col + 1])
+
+        def on_scalar(n, bb):
+            s, e = experts[n]
+            col = (s - 1) * E + e
+            if n not in gated_tiles:
+                gated_tiles[n] = gated_pool.tile([P, B_BLOCKS, U], F32, name="gated")
+            nc.scalar.activation(
+                out=gated_tiles[n][:, bb, :],
+                in_=hidden_t[(n, bb)][:],
+                func=ACT.Copy,
+                scale=g_share[:, bb, col : col + 1],
+            )
+
+        last_added = max(n for n in range(last_gated + 1) if not is_direct(n))
+
+        def add_transposed(n):
+            for ub in range(U_BLOCKS):
+                for bb in range(B_BLOCKS):
+                    place = (ub % 2) * B_BLOCKS + bb
+                    nc.tensor.matmul(
+                        out=acc[ub // 2][:, place * P : (place + 1) * P],
+                        lhsT=gated_tiles[n][:, bb, ub * P : (ub + 1) * P],
+                        rhs=ident[:],
+                        start=(n == 0 and place == 0),
+                        stop=(n == last_added and place == 2 * B_BLOCKS - 1),
+                        is_transpose=True,
+                    )
+
+        def turn_back():
+            acc_sb = gated_pool.tile([P, 2, U], F32, name="gated")
+            nc.scalar.copy(out=acc_sb[:, 0, :], in_=acc[0][:])
+            nc.scalar.copy(out=acc_sb[:, 1, :], in_=acc[1][:])
             for bb in range(B_BLOCKS):
-                h_t = psum_t.tile([P, U], F32, name="h_t")
+                back = psum_t.tile([P, U], F32, name="h_t")
                 for ub in range(U_BLOCKS):
+                    place = (ub % 2) * B_BLOCKS + bb
                     nc.tensor.transpose(
-                        out=h_t[:, ub * P : (ub + 1) * P],
-                        in_=hidden[(s, e)][:, ub, bb * P : (bb + 1) * P],
+                        out=back[:, ub * P : (ub + 1) * P],
+                        in_=acc_sb[:, ub // 2, place * P : (place + 1) * P],
                         identity=ident[:],
                     )
-                hidden_t[(s, e)].append(h_t)
+                nc.vector.tensor_tensor(
+                    out=shared_part[T][:, bb, :], in0=back[:], in1=shared_part[T][:, bb, :], op=ALU.add
+                )
 
         def finish(o):
             for bb in range(B_BLOCKS):
-                if o in early:
+                if o in shared_part:
                     nc.vector.tensor_tensor(
                         out=sums[o][:, bb, :], in0=sums[o][:, bb, :], in1=shared_part[o][:, bb, :], op=ALU.add
                     )
                 target = out_0[o] if o < T else out_1
                 nc.sync.dma_start(out=target[bb * P : (bb + 1) * P, :], in_=sums[o][:, bb, :])
-
-        def weighted_sums(s, e):
-            uses = [(s - 1, g_task, (s - 1) * G_TASK + e), (T, g_share, (s - 1) * E + e)]
-            for bb in range(B_BLOCKS):
-                for o, gates, col in uses:
-                    gate = gates[:, bb, col : col + 1]
-                    if terms[o] == 0:
-                        nc.vector.tensor_scalar_mul(out=sums[o][:, bb, :], in0=hidden_t[(s, e)][bb][:], scalar1=gate)
-                    else:
-                        nc.vector.scalar_tensor_tensor(
-                            out=sums[o][:, bb, :],
-                            in0=hidden_t[(s, e)][bb][:],
-                            scalar=gate,
-                            in1=sums[o][:, bb, :],
-                            op0=ALU.mult,
-                            op1=ALU.add,
-                        )
-            for o, gates, col in uses:
-                terms[o] += 1
 
         group_rows = {}
         group_parts = {}
@@ -319,7 +398,10 @@ def tile_plelayer_pa_kernel(
                     identity=ident[:],
                 )
             rows = rows_pool.tile([P, U], F32, name="rows")
-            nc.scalar.copy(out=rows[:], in_=turned_g[:])
+            if g % ROWS_V == ROWS_V - 1:
+                nc.vector.tensor_copy(out=rows[:], in_=turned_g[:])
+            else:
+                nc.scalar.copy(out=rows[:], in_=turned_g[:])
             group_rows[g] = rows
 
         def group_mix(g):
@@ -337,63 +419,89 @@ def tile_plelayer_pa_kernel(
             quad, place = divmod(g, QUAD)
             if place == 0:
                 part_tiles[quad] = part_pool.tile([P, QUAD, U], F32, name="part")
-            nc.scalar.copy(out=part_tiles[quad][:, place, :], in_=group_parts[g][:])
+            if g % PART_V == PART_V - 1:
+                nc.vector.tensor_copy(out=part_tiles[quad][:, place, :], in_=group_parts[g][:])
+            else:
+                nc.scalar.copy(out=part_tiles[quad][:, place, :], in_=group_parts[g][:])
             if place == QUAD - 1:
                 rows = slice(quad * QUAD * GB, (quad + 1) * QUAD * GB)
                 for o in range(SETS):
                     target = out_0[o] if o < T else out_1
-                    nc.gpsimd.dma_start(
+                    nc.sync.dma_start(
                         out=target[rows, :].rearrange("(q c) u -> c q u", c=GB),
                         in_=part_tiles[quad][o * GB : (o + 1) * GB, :, :],
                     )
             if g == N_GROUPS - 1:
                 for o in range(SETS):
                     source = out_0[o] if o < T else out_1
-                    target = shared_part[o] if o in early else sums[o]
-                    nc.gpsimd.dma_start(out=target[:], in_=source.rearrange("(bb p) u -> p bb u", p=P))
+                    target = shared_part[o] if o in shared_part else sums[o]
+                    nc.sync.dma_start(out=target[:], in_=source.rearrange("(bb p) u -> p bb u", p=P))
+
+        units = [(s, eg, ub) for s in range(1, SETS) for eg in range(GROUPS) for ub in range(U_BLOCKS)]
+        made = {"count": 0, "piece": 0}
+
+        def next_unit(engine):
+            if made["count"] < len(units):
+                regroup(*units[made["count"]], engine)
+                quantise(*units[made["count"]])
+                made["count"] += 1
 
         for ub in range(U_BLOCKS):
             regroup(0, 0, ub, "V")
             regroup(0, 1, ub, "S")
+            quantise(0, 0, ub)
             if ub > 0:
-                quantise(0, 0, ub - 1)
                 quantise(0, 1, ub - 1)
-        quantise(0, 0, U_BLOCKS - 1)
         quantise(0, 1, U_BLOCKS - 1)
-        set_1 = [(1, eg, ub) for eg in range(GROUPS) for ub in range(U_BLOCKS)]
         for e in range(E):
             multiply(0, e)
             bias_relu(0, e)
-            regroup(*set_1[e], "V")
-            if e > 0:
-                quantise(*set_1[e - 1])
-        quantise(*set_1[E - 1])
+            if e < U_BLOCKS:
+                next_unit("V")
+        make_mixer()
 
-        later = [(s, eg, ub) for s in range(2, SETS) for eg in range(GROUPS) for ub in range(U_BLOCKS)]
-        experts = [(1 + t, e) for t in range(T) for e in range(E)]
-        for i in range(N_TASK_EXPERTS + 2):
+        group_turn(0)
+        for g in range(N_GROUPS):
+            if g + 1 < N_GROUPS:
+                group_turn(g + 1)
+            group_mix(g)
+            group_out(g)
+            if g % AHEAD_EVERY != AHEAD_EVERY - 1:
+                next_unit("V")
+
+        finished = []
+        for i in range(N_TASK_EXPERTS + ADD_LAG + 1):
+            if 2 <= i < N_TASK_EXPERTS + 2:
+                if S_FIRST and not is_direct(i - 2):
+                    on_scalar(i - 2, 0)
+                    on_scalar(i - 2, 1)
+                    on_vector(i - 2, 0)
+                    on_vector(i - 2, 1)
+                else:
+                    on_vector(i - 2, 0)
+                    if not is_direct(i - 2):
+                        on_scalar(i - 2, 1)
+                        on_scalar(i - 2, 0)
+                    on_vector(i - 2, 1)
+            if 1 <= i <= N_TASK_EXPERTS:
+                transpose(i - 1, 0)
             if i < N_TASK_EXPERTS:
                 multiply(*experts[i])
                 bias_relu(*experts[i])
             if 1 <= i <= N_TASK_EXPERTS:
-                transpose(*experts[i - 1])
-            for g in range(PER_STEP * i, PER_STEP * (i + 1)):
-                if g < N_GROUPS:
-                    group_turn(g)
-                if 0 <= g - PER_STEP < N_GROUPS:
-                    group_mix(g - PER_STEP)
-                if 0 <= g - 2 * PER_STEP < N_GROUPS:
-                    group_out(g - 2 * PER_STEP)
-            if i >= 2:
-                weighted_sums(*experts[i - 2])
-                s, e = experts[i - 2]
-                if e == E - 1 and s - 1 >= LATE:
-                    finish(s - 1)
-                if i - 2 == FINISH_EARLY:
-                    for o in range(LATE):
-                        finish(o)
-            if 3 <= i < 3 + len(later):
-                quantise(*later[i - 3])
-            if 1 <= i < 1 + len(later):
-                regroup(*later[i - 1], "V" if i % V_EVERY == 0 else "S")
+                transpose(i - 1, 1)
+            if ADD_LAG <= i and i - ADD_LAG <= last_gated and not is_direct(i - ADD_LAG):
+                add_transposed(i - ADD_LAG)
+            if i - ADD_LAG == last_gated:
+                turn_back()
+            for repeat in range(PIECES_A_STEP):
+                if made["count"] < len(units):
+                    regroup(*units[made["count"]], "V", made["piece"], PIECES)
+                    made["piece"] += 1
+                    if made["piece"] == PIECES:
+                        quantise(*units[made["count"]])
+                        made["count"] += 1
+                        made["piece"] = 0
+            if i >= 2 and (i - 2) % E == E - 1:
+                finish((i - 2) // E)
         finish(T)

@@ -39,7 +39,7 @@ S_UNITS_EVERY = 3
 ROWS_V = 100
 PART_V = 100
 FINISH_AT = 20
-MANUAL = 1
+MANUAL = 0
 AHEAD_EVERY = 8
 PIECES = 4
 PIECES_A_STEP = 2

@@ -30,7 +30,7 @@ GB = 16
 N_GROUPS = B // GB
 O_SLOTS = P // GB
 QUAD = 4
-DIRECT = 2
+DIRECT = 1
 ADD_LAG = 3
 GROUP_FIRST = 1
 UNIT_LEAD = 5
@@ -39,10 +39,11 @@ S_UNITS_EVERY = 3
 ROWS_V = 100
 PART_V = 100
 FINISH_AT = 20
-MANUAL = 0
+MANUAL = 1
 AHEAD_EVERY = 8
-PIECES = 4
-PIECES_A_STEP = 2
+G_STEPS = 2
+G_PIECES = 1
+SPATH_EVERY = 2
 S_FIRST = 1
 DIRECT_EVERY = 1000
 Z_BUFS = 3
@@ -62,7 +63,8 @@ def tile_plelayer_pa_kernel(
             ctx.enter_context(tc.manual_schedule())
         const = ctx.enter_context(tc.tile_pool(name="const", bufs=1))
         raw_pool = ctx.enter_context(tc.tile_pool(name="raw", bufs=6))
-        unit_pool = ctx.enter_context(tc.tile_pool(name="unit", bufs=4))
+        unit_pool = ctx.enter_context(tc.tile_pool(name="unit", bufs=3))
+        held_pool = ctx.enter_context(tc.tile_pool(name="held", bufs=1))
         codes_pool = ctx.enter_context(tc.tile_pool(name="codes", bufs=5))
         h_pool = ctx.enter_context(tc.tile_pool(name="h", bufs=3))
         rows_pool = ctx.enter_context(tc.tile_pool(name="rows", bufs=2))
@@ -109,9 +111,10 @@ def tile_plelayer_pa_kernel(
                 nc.sync.dma_start(out=raw[:], in_=rows[:, :, ub * CHUNK : (ub + 1) * CHUNK])
                 raw_tiles[(s, ub)] = raw
 
-        def regroup(s, eg, ub, engine, piece=0, pieces=1):
+        def regroup(s, eg, ub, engine, piece=0, pieces=1, hold=False):
             if piece == 0:
-                unit_tiles[(s, eg, ub)] = unit_pool.tile([P, E_GROUP, P, PACK], BF16, name="unit", align_bytes=64)
+                pool = held_pool if (engine == "G" or hold) else unit_pool
+                unit_tiles[(s, eg, ub)] = pool.tile([P, E_GROUP, P, PACK], BF16, name="unit", align_bytes=64)
             grouped = unit_tiles[(s, eg, ub)]
             span = slice(piece * (P // pieces), (piece + 1) * (P // pieces))
             source = raw_tiles[(s, ub)][:].rearrange("p t (u e) -> p u t e", e=E)
@@ -119,8 +122,17 @@ def tile_plelayer_pa_kernel(
             target = grouped[:].rearrange("p i u t -> p u t i")[:, span]
             if engine == "V":
                 nc.vector.tensor_copy(out=target, in_=source)
-            else:
+            elif engine == "S":
                 nc.scalar.copy(out=target, in_=source)
+            else:
+                nc.gpsimd.tensor_scalar(
+                    out=target.rearrange("p u t i -> p u i t"),
+                    in0=source.rearrange("p u t i -> p u i t"),
+                    scalar1=1.0,
+                    scalar2=0.0,
+                    op0=ALU.mult,
+                    op1=ALU.add,
+                )
             if piece == pieces - 1:
                 readers[(s, ub)] = readers.get((s, ub), 0) + 1
                 if readers[(s, ub)] == GROUPS:
@@ -268,7 +280,7 @@ def tile_plelayer_pa_kernel(
         last_gated = N_TASK_EXPERTS - DIRECT - 1
 
         def is_direct(n):
-            return n > last_gated or n % DIRECT_EVERY == DIRECT_EVERY - 1
+            return n > last_gated or n % SPATH_EVERY != 0
 
         def multiply(s, e):
             eg, i = divmod(e, E_GROUP)
@@ -440,9 +452,9 @@ def tile_plelayer_pa_kernel(
         units = [(s, eg, ub) for s in range(1, SETS) for eg in range(GROUPS) for ub in range(U_BLOCKS)]
         made = {"count": 0, "piece": 0}
 
-        def next_unit(engine):
+        def next_unit(engine, hold=False):
             if made["count"] < len(units):
-                regroup(*units[made["count"]], engine)
+                regroup(*units[made["count"]], engine, 0, 1, hold)
                 quantise(*units[made["count"]])
                 made["count"] += 1
 
@@ -467,10 +479,19 @@ def tile_plelayer_pa_kernel(
             group_mix(g)
             group_out(g)
             if g % AHEAD_EVERY != AHEAD_EVERY - 1:
-                next_unit("V")
+                next_unit("V", g == N_GROUPS - 1 - (1 if (N_GROUPS - 1) % AHEAD_EVERY == AHEAD_EVERY - 1 else 0))
 
         finished = []
         for i in range(N_TASK_EXPERTS + ADD_LAG + 1):
+            if i % G_STEPS == 0:
+                if made["piece"] == 1:
+                    quantise(*units[made["count"]])
+                    made["count"] += 1
+                    made["piece"] = 0
+                if made["count"] < len(units):
+                    for piece in range(G_PIECES):
+                        regroup(*units[made["count"]], "G", piece, G_PIECES)
+                    made["piece"] = 1
             if 2 <= i < N_TASK_EXPERTS + 2:
                 if S_FIRST and not is_direct(i - 2):
                     on_scalar(i - 2, 0)
@@ -494,14 +515,6 @@ def tile_plelayer_pa_kernel(
                 add_transposed(i - ADD_LAG)
             if i - ADD_LAG == last_gated:
                 turn_back()
-            for repeat in range(PIECES_A_STEP):
-                if made["count"] < len(units):
-                    regroup(*units[made["count"]], "V", made["piece"], PIECES)
-                    made["piece"] += 1
-                    if made["piece"] == PIECES:
-                        quantise(*units[made["count"]])
-                        made["count"] += 1
-                        made["piece"] = 0
             if i >= 2 and (i - 2) % E == E - 1:
                 finish((i - 2) // E)
         finish(T)

@@ -59,8 +59,6 @@ def tile_plelayer_pa_kernel(
 ):
     nc = tc.nc
     with ExitStack() as ctx:
-        if MANUAL:
-            ctx.enter_context(tc.manual_schedule())
         const = ctx.enter_context(tc.tile_pool(name="const", bufs=1))
         raw_pool = ctx.enter_context(tc.tile_pool(name="raw", bufs=6))
         unit_pool = ctx.enter_context(tc.tile_pool(name="unit", bufs=3))
@@ -482,6 +480,8 @@ def tile_plelayer_pa_kernel(
                 next_unit("V", g == N_GROUPS - 1 - (1 if (N_GROUPS - 1) % AHEAD_EVERY == AHEAD_EVERY - 1 else 0))
 
         finished = []
+        if MANUAL:
+            ctx.enter_context(tc.manual_schedule())
         for i in range(N_TASK_EXPERTS + ADD_LAG + 1):
             if i % G_STEPS == 0:
                 if made["piece"] == 1:

@@ -43,11 +43,11 @@ MANUAL = 1
 AHEAD_EVERY = 8
 G_STEPS = 2
 G_PIECES = 1
-SPATH_EVERY = 2
+SPATH_EVERY = 1
 S_FIRST = 1
 DIRECT_EVERY = 1000
 Z_BUFS = 3
-HT_BUFS = 3
+HT_BUFS = 4
 
 FLOPS = 2 * B * D * U * E * SETS
 
@@ -273,7 +273,7 @@ def tile_plelayer_pa_kernel(
         products = {}
         hidden = {}
         hidden_t = {}
-        acc = [psum_acc.tile([P, U], F32, name="acc_%d" % half) for half in range(2)]
+        acc = psum_acc.tile([P, U], F32, name="acc")
         gated_tiles = {}
         last_gated = N_TASK_EXPERTS - DIRECT - 1
 
@@ -338,17 +338,16 @@ def tile_plelayer_pa_kernel(
             s, e = experts[n]
             col = (s - 1) * G_TASK + e
             add_term(s - 1, bb, hidden_t[(n, bb)][:], g_task[:, bb, col : col + 1])
-            if is_direct(n):
+            if is_direct(n) or bb == 1:
                 col = (s - 1) * E + e
                 add_term(T, bb, hidden_t[(n, bb)][:], g_share[:, bb, col : col + 1])
 
         def on_scalar(n, bb):
             s, e = experts[n]
             col = (s - 1) * E + e
-            if n not in gated_tiles:
-                gated_tiles[n] = gated_pool.tile([P, B_BLOCKS, U], F32, name="gated")
+            gated_tiles[n] = gated_pool.tile([P, U], F32, name="gated")
             nc.scalar.activation(
-                out=gated_tiles[n][:, bb, :],
+                out=gated_tiles[n][:],
                 in_=hidden_t[(n, bb)][:],
                 func=ACT.Copy,
                 scale=g_share[:, bb, col : col + 1],
@@ -358,33 +357,26 @@ def tile_plelayer_pa_kernel(
 
         def add_transposed(n):
             for ub in range(U_BLOCKS):
-                for bb in range(B_BLOCKS):
-                    place = (ub % 2) * B_BLOCKS + bb
-                    nc.tensor.matmul(
-                        out=acc[ub // 2][:, place * P : (place + 1) * P],
-                        lhsT=gated_tiles[n][:, bb, ub * P : (ub + 1) * P],
-                        rhs=ident[:],
-                        start=(n == 0 and place == 0),
-                        stop=(n == last_added and place == 2 * B_BLOCKS - 1),
-                        is_transpose=True,
-                    )
+                nc.tensor.matmul(
+                    out=acc[:, ub * P : (ub + 1) * P],
+                    lhsT=gated_tiles[n][:, ub * P : (ub + 1) * P],
+                    rhs=ident[:],
+                    start=(n == 0 and ub == 0),
+                    stop=(n == last_added and ub == U_BLOCKS - 1),
+                    is_transpose=True,
+                )
 
         def turn_back():
-            acc_sb = gated_pool.tile([P, 2, U], F32, name="gated")
-            nc.scalar.copy(out=acc_sb[:, 0, :], in_=acc[0][:])
-            nc.scalar.copy(out=acc_sb[:, 1, :], in_=acc[1][:])
-            for bb in range(B_BLOCKS):
-                back = psum_t.tile([P, U], F32, name="h_t")
-                for ub in range(U_BLOCKS):
-                    place = (ub % 2) * B_BLOCKS + bb
-                    nc.tensor.transpose(
-                        out=back[:, ub * P : (ub + 1) * P],
-                        in_=acc_sb[:, ub // 2, place * P : (place + 1) * P],
-                        identity=ident[:],
-                    )
-                nc.vector.tensor_tensor(
-                    out=shared_part[T][:, bb, :], in0=back[:], in1=shared_part[T][:, bb, :], op=ALU.add
+            acc_sb = gated_pool.tile([P, U], F32, name="gated")
+            nc.scalar.copy(out=acc_sb[:], in_=acc[:])
+            back = psum_t.tile([P, U], F32, name="h_t")
+            for ub in range(U_BLOCKS):
+                nc.tensor.transpose(
+                    out=back[:, ub * P : (ub + 1) * P], in_=acc_sb[:, ub * P : (ub + 1) * P], identity=ident[:]
                 )
+            nc.vector.tensor_tensor(
+                out=shared_part[T][:, 0, :], in0=back[:], in1=shared_part[T][:, 0, :], op=ALU.add
+            )
 
         def finish(o):
             for bb in range(B_BLOCKS):
@@ -451,17 +443,17 @@ def tile_plelayer_pa_kernel(
         made = {"count": 0, "piece": 0}
 
         def next_unit(engine, hold=False):
-            if made["count"] < len(units):
-                regroup(*units[made["count"]], engine, 0, 1, hold)
-                quantise(*units[made["count"]])
-                made["count"] += 1
+            regroup(*units[made["count"]], engine, 0, 1, hold)
+            if made["count"] > 0:
+                quantise(*units[made["count"] - 1])
+            made["count"] += 1
 
         for ub in range(U_BLOCKS):
             regroup(0, 0, ub, "V")
             regroup(0, 1, ub, "S")
-            quantise(0, 0, ub)
             if ub > 0:
                 quantise(0, 1, ub - 1)
+            quantise(0, 0, ub)
         quantise(0, 1, U_BLOCKS - 1)
         for e in range(E):
             multiply(0, e)
@@ -479,6 +471,8 @@ def tile_plelayer_pa_kernel(
             if g % AHEAD_EVERY != AHEAD_EVERY - 1:
                 next_unit("V", g == N_GROUPS - 1 - (1 if (N_GROUPS - 1) % AHEAD_EVERY == AHEAD_EVERY - 1 else 0))
 
+        quantise(*units[made["count"] - 1])
+
         finished = []
         if MANUAL:
             ctx.enter_context(tc.manual_schedule())
@@ -493,17 +487,10 @@ def tile_plelayer_pa_kernel(
                         regroup(*units[made["count"]], "G", piece, G_PIECES)
                     made["piece"] = 1
             if 2 <= i < N_TASK_EXPERTS + 2:
-                if S_FIRST and not is_direct(i - 2):
+                if not is_direct(i - 2):
                     on_scalar(i - 2, 0)
-                    on_scalar(i - 2, 1)
-                    on_vector(i - 2, 0)
-                    on_vector(i - 2, 1)
-                else:
-                    on_vector(i - 2, 0)
-                    if not is_direct(i - 2):
-                        on_scalar(i - 2, 1)
-                        on_scalar(i - 2, 0)
-                    on_vector(i - 2, 1)
+                on_vector(i - 2, 1)
+                on_vector(i - 2, 0)
             if 1 <= i <= N_TASK_EXPERTS:
                 transpose(i - 1, 0)
             if i < N_TASK_EXPERTS:

@@ -491,12 +491,11 @@ def tile_plelayer_pa_kernel(
                     on_scalar(i - 2, 0)
                 on_vector(i - 2, 1)
                 on_vector(i - 2, 0)
-            if 1 <= i <= N_TASK_EXPERTS:
-                transpose(i - 1, 0)
             if i < N_TASK_EXPERTS:
                 multiply(*experts[i])
                 bias_relu(*experts[i])
             if 1 <= i <= N_TASK_EXPERTS:
+                transpose(i - 1, 0)
                 transpose(i - 1, 1)
             if ADD_LAG <= i and i - ADD_LAG <= last_gated and not is_direct(i - ADD_LAG):
                 add_transposed(i - ADD_LAG)

@@ -72,13 +72,6 @@ def tile_plelayer_pa_kernel(
         psum_t = ctx.enter_context(tc.psum_pool(name="psum_t", bufs=HT_BUFS))
         psum_acc = ctx.enter_context(tc.psum_pool(name="psum_acc", bufs=1))
 
-        x_sb = const.tile([P, B_BLOCKS, D], BF16)
-        nc.sync.dma_start(out=x_sb[:], in_=x.rearrange("(bb p) d -> p bb d", p=P))
-
-        bias_bf = const.tile([P, SETS, U_BLOCKS, E], BF16)
-        nc.scalar.dma_start(out=bias_bf[:, 0], in_=ebs0.rearrange("(ub p) e -> p ub e", p=P))
-        nc.scalar.dma_start(out=bias_bf[:, 1:SETS], in_=eb0.rearrange("t (ub p) e -> p t ub e", p=P))
-
         pre_task = const.tile([P, B_BLOCKS, T, G_TASK], BF16)
         for bb in range(B_BLOCKS):
             nc.scalar.dma_start(
@@ -87,10 +80,14 @@ def tile_plelayer_pa_kernel(
             )
         pre_share = const.tile([P, B_BLOCKS, G_SHARE], BF16)
         nc.scalar.dma_start(out=pre_share[:], in_=sgate_pre.rearrange("(bb p) g -> p bb g", p=P))
-        gb_task = const.tile([P, T * G_TASK], BF16)
-        nc.scalar.dma_start(out=gb_task[:], in_=gb0.rearrange("t g -> (t g)").partition_broadcast(P))
-        gb_share = const.tile([P, G_SHARE], BF16)
-        nc.scalar.dma_start(out=gb_share[:], in_=gbs.partition_broadcast(P))
+        gate_row = const.tile([P, T * G_TASK + G_SHARE], BF16)
+        nc.gpsimd.memset(gate_row[:], 0.0)
+        nc.scalar.dma_start(out=gate_row[0:1, 0 : T * G_TASK], in_=gb0.rearrange("t g -> (t g)").unsqueeze(0))
+        nc.scalar.dma_start(out=gate_row[0:1, T * G_TASK :], in_=gbs.unsqueeze(0))
+        ones = const.tile([P, P], BF16)
+        nc.gpsimd.memset(ones[:], 1.0)
+        x_sb = const.tile([P, B_BLOCKS, D], BF16)
+        bias_bf = const.tile([P, SETS, U_BLOCKS, E], BF16)
 
         raw_tiles = {}
         code_tiles = {}
@@ -106,7 +103,13 @@ def tile_plelayer_pa_kernel(
                 w = ews0 if s == 0 else ew0[s - 1]
                 rows = w.rearrange("(p t) u e -> p t (u e)", t=PACK)
                 raw = raw_pool.tile([P, PACK, CHUNK], BF16, name="raw")
-                nc.sync.dma_start(out=raw[:], in_=rows[:, :, ub * CHUNK : (ub + 1) * CHUNK])
+                pieces = 2 if loaded["count"] == 1 else 1
+                width = CHUNK // pieces
+                for piece in range(pieces):
+                    nc.sync.dma_start(
+                        out=raw[:, :, piece * width : (piece + 1) * width],
+                        in_=rows[:, :, ub * CHUNK + piece * width : ub * CHUNK + (piece + 1) * width],
+                    )
                 raw_tiles[(s, ub)] = raw
 
         def regroup(s, eg, ub, engine, piece=0, pieces=1, hold=False):
@@ -124,8 +127,8 @@ def tile_plelayer_pa_kernel(
                 nc.scalar.copy(out=target, in_=source)
             else:
                 nc.gpsimd.tensor_scalar(
-                    out=target.rearrange("p u t i -> p u i t"),
-                    in0=source.rearrange("p u t i -> p u i t"),
+                    out=target,
+                    in0=source,
                     scalar1=1.0,
                     scalar2=0.0,
                     op0=ALU.mult,
@@ -149,29 +152,15 @@ def tile_plelayer_pa_kernel(
                 in_=unit_tiles[(s, eg, ub)][:].rearrange("p i u t -> p (i u t)"),
             )
 
-        for first in range(6):
-            load_next()
-
-        ident = const.tile([P, P], F32)
-        make_identity(nc, ident[:])
-        x_words = x_sb[:].bitcast(F32).rearrange("p bb (w j) -> p bb j w", j=2)
-        x_t = psum_t.tile([P, 2, B], F32, tag="h_t")
-        for bb in range(B_BLOCKS):
-            for j in range(2):
-                nc.tensor.transpose(
-                    out=x_t[:, j, bb * P : (bb + 1) * P], in_=x_words[:, bb, j, :], identity=ident[:]
-                )
-        x_grouped = const.tile([P, B, PACK], BF16, align_bytes=64)
-        nc.vector.tensor_copy(out=x_grouped[:].bitcast(F32), in_=x_t[:].rearrange("p j b -> p b j"))
-        x_codes = const.tile([P, B], U32, align_bytes=64)
-        x_scales = const.tile([P, B], U8, align_bytes=64)
-        nc.vector.quantize_mx(
-            out=x_codes[:].bitcast(FP8X4),
-            scales=x_scales[:],
-            in_=x_grouped[:].rearrange("p b t -> p (b t)"),
-        )
-        bias_f = const.tile([P, SETS, U_BLOCKS, E], F32)
-        nc.vector.tensor_copy(out=bias_f[:], in_=bias_bf[:])
+        load_next()
+        nc.sync.dma_start(out=x_sb[:], in_=x.rearrange("(bb p) d -> p bb d", p=P))
+        load_next()
+        load_next()
+        nc.sync.dma_start(out=bias_bf[:, 0], in_=ebs0.rearrange("(ub p) e -> p ub e", p=P))
+        load_next()
+        nc.sync.dma_start(out=bias_bf[:, 1:SETS], in_=eb0.rearrange("t (ub p) e -> p t ub e", p=P))
+        load_next()
+        load_next()
 
         g_task = const.tile([P, B_BLOCKS, T * G_TASK], F32)
         g_share = const.tile([P, B_BLOCKS, G_SHARE], F32)
@@ -195,23 +184,46 @@ def tile_plelayer_pa_kernel(
                 out=logits, in0=logits, in1=inverse[:].unsqueeze(2).to_broadcast(wide), op=ALU.mult
             )
 
+        gate_bias = psum_t.tile([P, T * G_TASK + G_SHARE], F32, tag="h_t")
+        nc.tensor.matmul(out=gate_bias[:], lhsT=ones[:], rhs=gate_row[:], start=True, stop=True)
         task_rows = g_task[:].rearrange("p bb (t g) -> p (bb t) g", g=G_TASK)
         nc.vector.tensor_tensor(
             out=g_task[:],
             in0=pre_task[:].rearrange("p bb t g -> p bb (t g)"),
-            in1=gb_task[:].unsqueeze(1).to_broadcast([P, B_BLOCKS, T * G_TASK]),
+            in1=gate_bias[:, 0 : T * G_TASK].unsqueeze(1).to_broadcast([P, B_BLOCKS, T * G_TASK]),
             op=ALU.add,
         )
         softmax_head(task_rows, B_BLOCKS * T, G_TASK, "task")
         nc.vector.tensor_tensor(
             out=g_share[:],
             in0=pre_share[:],
-            in1=gb_share[:].unsqueeze(1).to_broadcast([P, B_BLOCKS, G_SHARE]),
+            in1=gate_bias[:, T * G_TASK :].unsqueeze(1).to_broadcast([P, B_BLOCKS, G_SHARE]),
             op=ALU.add,
         )
         softmax_head(g_share[:], B_BLOCKS, G_SHARE, "share")
         softmax_tail(task_rows, B_BLOCKS * T, G_TASK, "task")
         softmax_tail(g_share[:], B_BLOCKS, G_SHARE, "share")
+
+        ident = const.tile([P, P], F32)
+        make_identity(nc, ident[:])
+        x_words = x_sb[:].bitcast(F32).rearrange("p bb (w j) -> p bb j w", j=2)
+        x_t = psum_t.tile([P, 2, B], F32, tag="h_t")
+        for bb in range(B_BLOCKS):
+            for j in range(2):
+                nc.tensor.transpose(
+                    out=x_t[:, j, bb * P : (bb + 1) * P], in_=x_words[:, bb, j, :], identity=ident[:]
+                )
+        x_grouped = const.tile([P, B, PACK], BF16, align_bytes=64)
+        nc.scalar.copy(out=x_grouped[:].bitcast(F32), in_=x_t[:].rearrange("p j b -> p b j"))
+        x_codes = const.tile([P, B], U32, align_bytes=64)
+        x_scales = const.tile([P, B], U8, align_bytes=64)
+        nc.vector.quantize_mx(
+            out=x_codes[:].bitcast(FP8X4),
+            scales=x_scales[:],
+            in_=x_grouped[:].rearrange("p b t -> p (b t)"),
+        )
+        bias_f = const.tile([P, SETS, U_BLOCKS, E], F32)
+        nc.gpsimd.tensor_copy(out=bias_f[:], in_=bias_bf[:])
 
         mixer = const.tile([P, N_GROUPS, O_SLOTS, GB], F32)
         nc.gpsimd.memset(mixer[:], 0.0)
@@ -259,13 +271,11 @@ def tile_plelayer_pa_kernel(
 
         experts = [(1 + t, e) for t in range(T) for e in range(E)]
         sums = [const.tile([P, B_BLOCKS, U], F32, name="sum_%d" % o) for o in range(SETS)]
-        shared_part = {}
-        for o in (0, T):
-            shared_part[o] = const.tile([P, B_BLOCKS, U], F32, name="shared_part_%d" % o)
+        late_part = const.tile([P, U], F32)
         terms = {}
-        for o in range(1, T):
+        for o in range(SETS):
             for bb in range(B_BLOCKS):
-                terms[(o, bb)] = 1
+                terms[(o, bb)] = 0 if (o, bb) == (0, 0) else 1
         hidden_s = []
         for ub in range(U_BLOCKS):
             block = gated_pool.tile([P, N_GROUPS, E, GB], F32, name="gated")
@@ -374,15 +384,13 @@ def tile_plelayer_pa_kernel(
                 nc.tensor.transpose(
                     out=back[:, ub * P : (ub + 1) * P], in_=acc_sb[:, ub * P : (ub + 1) * P], identity=ident[:]
                 )
-            nc.vector.tensor_tensor(
-                out=shared_part[T][:, 0, :], in0=back[:], in1=shared_part[T][:, 0, :], op=ALU.add
-            )
+            nc.vector.tensor_tensor(out=sums[T][:, 0, :], in0=back[:], in1=sums[T][:, 0, :], op=ALU.add)
 
         def finish(o):
             for bb in range(B_BLOCKS):
-                if o in shared_part:
+                if (o, bb) == (0, 0):
                     nc.vector.tensor_tensor(
-                        out=sums[o][:, bb, :], in0=sums[o][:, bb, :], in1=shared_part[o][:, bb, :], op=ALU.add
+                        out=sums[o][:, bb, :], in0=sums[o][:, bb, :], in1=late_part[:], op=ALU.add
                     )
                 target = out_0[o] if o < T else out_1
                 nc.sync.dma_start(out=target[bb * P : (bb + 1) * P, :], in_=sums[o][:, bb, :])
@@ -433,11 +441,12 @@ def tile_plelayer_pa_kernel(
                         out=target[rows, :].rearrange("(q c) u -> c q u", c=GB),
                         in_=part_tiles[quad][o * GB : (o + 1) * GB, :, :],
                     )
-            if g == N_GROUPS - 1:
+            if g % (N_GROUPS // B_BLOCKS) == N_GROUPS // B_BLOCKS - 1:
+                bb = g // (N_GROUPS // B_BLOCKS)
                 for o in range(SETS):
                     source = out_0[o] if o < T else out_1
-                    target = shared_part[o] if o in shared_part else sums[o]
-                    nc.sync.dma_start(out=target[:], in_=source.rearrange("(bb p) u -> p bb u", p=P))
+                    target = late_part[:] if (o, bb) == (0, 0) else sums[o][:, bb, :]
+                    nc.sync.dma_start(out=target, in_=source[bb * P : (bb + 1) * P, :])
 
         units = [(s, eg, ub) for s in range(1, SETS) for eg in range(GROUPS) for ub in range(U_BLOCKS)]
         made = {"count": 0, "piece": 0}
@@ -449,8 +458,10 @@ def tile_plelayer_pa_kernel(
             made["count"] += 1
 
         for ub in range(U_BLOCKS):
-            regroup(0, 0, ub, "V")
-            regroup(0, 1, ub, "S")
+            pieces = 2 if ub == 0 else 1
+            for piece in range(pieces):
+                regroup(0, 0, ub, "V", piece, pieces)
+                regroup(0, 1, ub, "S", piece, pieces)
             if ub > 0:
                 quantise(0, 1, ub - 1)
             quantise(0, 0, ub)
@@ -462,12 +473,13 @@ def tile_plelayer_pa_kernel(
                 next_unit("V")
         make_mixer()
 
-        group_turn(0)
+        order = list(range(N_GROUPS // B_BLOCKS, N_GROUPS)) + list(range(N_GROUPS // B_BLOCKS))
+        group_turn(order[0])
         for g in range(N_GROUPS):
             if g + 1 < N_GROUPS:
-                group_turn(g + 1)
-            group_mix(g)
-            group_out(g)
+                group_turn(order[g + 1])
+            group_mix(order[g])
+            group_out(order[g])
             if g % AHEAD_EVERY != AHEAD_EVERY - 1:
                 next_unit("V", g == N_GROUPS - 1 - (1 if (N_GROUPS - 1) % AHEAD_EVERY == AHEAD_EVERY - 1 else 0))
 

@@ -21,33 +21,21 @@ U_BLOCKS = U // P
 E_GROUP = 4
 GROUPS = E // E_GROUP
 UNIT_WORDS = E_GROUP * P
-UNIT_COLS = UNIT_WORDS * PACK
 CHUNK = P * E
 G_TASK = 2 * E
 G_SHARE = SETS * E
 N_TASK_EXPERTS = T * E
 GB = 16
-N_GROUPS = B // GB
+N_ROWGROUPS = B // GB
 O_SLOTS = P // GB
 QUAD = 4
-DIRECT = 1
+RAW_BUFS = 6
+RELU_UNITS = 4
+AHEAD = 19
+G_CUT = 112
+Q_FIRST = 3
+Q_LAST = 27
 ADD_LAG = 3
-GROUP_FIRST = 1
-UNIT_LEAD = 5
-S_UNITS_FROM = 100
-S_UNITS_EVERY = 3
-ROWS_V = 100
-PART_V = 100
-FINISH_AT = 20
-MANUAL = 1
-AHEAD_EVERY = 8
-G_STEPS = 2
-G_PIECES = 1
-SPATH_EVERY = 1
-S_FIRST = 1
-DIRECT_EVERY = 1000
-Z_BUFS = 3
-HT_BUFS = 4
 
 FLOPS = 2 * B * D * U * E * SETS
 
@@ -60,16 +48,16 @@ def tile_plelayer_pa_kernel(
     nc = tc.nc
     with ExitStack() as ctx:
         const = ctx.enter_context(tc.tile_pool(name="const", bufs=1))
-        raw_pool = ctx.enter_context(tc.tile_pool(name="raw", bufs=6))
+        raw_pool = ctx.enter_context(tc.tile_pool(name="raw", bufs=RAW_BUFS))
         unit_pool = ctx.enter_context(tc.tile_pool(name="unit", bufs=3))
         held_pool = ctx.enter_context(tc.tile_pool(name="held", bufs=1))
         codes_pool = ctx.enter_context(tc.tile_pool(name="codes", bufs=5))
         h_pool = ctx.enter_context(tc.tile_pool(name="h", bufs=3))
         rows_pool = ctx.enter_context(tc.tile_pool(name="rows", bufs=2))
         part_pool = ctx.enter_context(tc.tile_pool(name="part", bufs=2))
-        gated_pool = ctx.enter_context(tc.tile_pool(name="gated", bufs=4))
-        psum_mx = ctx.enter_context(tc.psum_pool(name="psum_mx", bufs=Z_BUFS))
-        psum_t = ctx.enter_context(tc.psum_pool(name="psum_t", bufs=HT_BUFS))
+        gated_pool = ctx.enter_context(tc.tile_pool(name="gated", bufs=2))
+        psum_mx = ctx.enter_context(tc.psum_pool(name="psum_mx", bufs=3))
+        psum_t = ctx.enter_context(tc.psum_pool(name="psum_t", bufs=4))
         psum_acc = ctx.enter_context(tc.psum_pool(name="psum_acc", bufs=1))
 
         pre_task = const.tile([P, B_BLOCKS, T, G_TASK], BF16)
@@ -86,24 +74,28 @@ def tile_plelayer_pa_kernel(
         nc.scalar.dma_start(out=gate_row[0:1, T * G_TASK :], in_=gbs.unsqueeze(0))
         ones = const.tile([P, P], BF16)
         nc.gpsimd.memset(ones[:], 1.0)
+        bias_rows = const.tile([P, P * E], BF16)
+        nc.gpsimd.memset(bias_rows[:], 0.0)
+        nc.gpsimd.dma_start(out=bias_rows[0:U_BLOCKS, :], in_=ebs0.rearrange("(ub p) e -> ub (p e)", p=P))
+        nc.gpsimd.dma_start(
+            out=bias_rows[U_BLOCKS : SETS * U_BLOCKS, :], in_=eb0.rearrange("t (ub p) e -> (t ub) (p e)", p=P)
+        )
         x_sb = const.tile([P, B_BLOCKS, D], BF16)
-        bias_bf = const.tile([P, SETS, U_BLOCKS, E], BF16)
 
         raw_tiles = {}
         code_tiles = {}
         unit_tiles = {}
-        loads = [(s, ub) for s in range(SETS) for ub in range(U_BLOCKS)]
-        loaded = {"count": 0}
         readers = {}
+        loads = [(s, ub) for s in range(SETS) for ub in range(U_BLOCKS)]
+        units = [(s, eg, ub) for s in (1, 2) for ub in range(U_BLOCKS) for eg in range(GROUPS)]
+        units += [(s, eg, ub) for s in range(3, SETS) for eg in range(GROUPS) for ub in range(U_BLOCKS)]
 
-        def load_next():
-            if loaded["count"] < len(loads):
-                s, ub = loads[loaded["count"]]
-                loaded["count"] += 1
+        def load_next(pieces=1):
+            if loads:
+                s, ub = loads.pop(0)
                 w = ews0 if s == 0 else ew0[s - 1]
                 rows = w.rearrange("(p t) u e -> p t (u e)", t=PACK)
                 raw = raw_pool.tile([P, PACK, CHUNK], BF16, name="raw")
-                pieces = 2 if loaded["count"] == 1 else 1
                 width = CHUNK // pieces
                 for piece in range(pieces):
                     nc.sync.dma_start(
@@ -112,34 +104,29 @@ def tile_plelayer_pa_kernel(
                     )
                 raw_tiles[(s, ub)] = raw
 
-        def regroup(s, eg, ub, engine, piece=0, pieces=1, hold=False):
-            if piece == 0:
-                pool = held_pool if (engine == "G" or hold) else unit_pool
-                unit_tiles[(s, eg, ub)] = pool.tile([P, E_GROUP, P, PACK], BF16, name="unit", align_bytes=64)
-            grouped = unit_tiles[(s, eg, ub)]
-            span = slice(piece * (P // pieces), (piece + 1) * (P // pieces))
+        def regroup(unit, engine, first, last, held=False):
+            s, eg, ub = unit
+            if first == 0:
+                pool = held_pool if held else unit_pool
+                unit_tiles[unit] = pool.tile([P, E_GROUP, P, PACK], BF16, name="unit", align_bytes=64)
             source = raw_tiles[(s, ub)][:].rearrange("p t (u e) -> p u t e", e=E)
-            source = source[:, span, :, eg * E_GROUP : (eg + 1) * E_GROUP]
-            target = grouped[:].rearrange("p i u t -> p u t i")[:, span]
+            source = source[:, first:last, :, eg * E_GROUP : (eg + 1) * E_GROUP]
+            target = unit_tiles[unit][:].rearrange("p i u t -> p u t i")[:, first:last]
             if engine == "V":
                 nc.vector.tensor_copy(out=target, in_=source)
             elif engine == "S":
                 nc.scalar.copy(out=target, in_=source)
             else:
                 nc.gpsimd.tensor_scalar(
-                    out=target,
-                    in0=source,
-                    scalar1=1.0,
-                    scalar2=0.0,
-                    op0=ALU.mult,
-                    op1=ALU.add,
+                    out=target, in0=source, scalar1=1.0, scalar2=0.0, op0=ALU.mult, op1=ALU.add
                 )
-            if piece == pieces - 1:
+            if last == P:
                 readers[(s, ub)] = readers.get((s, ub), 0) + 1
                 if readers[(s, ub)] == GROUPS:
                     load_next()
 
-        def quantise(s, eg, ub):
+        def quantise(unit):
+            s, eg, ub = unit
             if (s, eg) not in code_tiles:
                 codes = codes_pool.tile([P, U_BLOCKS * UNIT_WORDS], U32, name="codes", align_bytes=64)
                 scales = codes_pool.tile([P, U_BLOCKS * UNIT_WORDS], U8, name="scales", align_bytes=64)
@@ -149,18 +136,13 @@ def tile_plelayer_pa_kernel(
             nc.vector.quantize_mx(
                 out=codes[:, cols].bitcast(FP8X4),
                 scales=scales[:, cols],
-                in_=unit_tiles[(s, eg, ub)][:].rearrange("p i u t -> p (i u t)"),
+                in_=unit_tiles[unit][:].rearrange("p i u t -> p (i u t)"),
             )
 
-        load_next()
+        load_next(pieces=2)
         nc.sync.dma_start(out=x_sb[:], in_=x.rearrange("(bb p) d -> p bb d", p=P))
-        load_next()
-        load_next()
-        nc.sync.dma_start(out=bias_bf[:, 0], in_=ebs0.rearrange("(ub p) e -> p ub e", p=P))
-        load_next()
-        nc.sync.dma_start(out=bias_bf[:, 1:SETS], in_=eb0.rearrange("t (ub p) e -> p t ub e", p=P))
-        load_next()
-        load_next()
+        for count in range(RAW_BUFS - 1):
+            load_next()
 
         g_task = const.tile([P, B_BLOCKS, T * G_TASK], F32)
         g_share = const.tile([P, B_BLOCKS, G_SHARE], F32)
@@ -184,7 +166,7 @@ def tile_plelayer_pa_kernel(
                 out=logits, in0=logits, in1=inverse[:].unsqueeze(2).to_broadcast(wide), op=ALU.mult
             )
 
-        gate_bias = psum_t.tile([P, T * G_TASK + G_SHARE], F32, tag="h_t")
+        gate_bias = psum_t.tile([P, T * G_TASK + G_SHARE], F32, name="h_t")
         nc.tensor.matmul(out=gate_bias[:], lhsT=ones[:], rhs=gate_row[:], start=True, stop=True)
         task_rows = g_task[:].rearrange("p bb (t g) -> p (bb t) g", g=G_TASK)
         nc.vector.tensor_tensor(
@@ -207,7 +189,7 @@ def tile_plelayer_pa_kernel(
         ident = const.tile([P, P], F32)
         make_identity(nc, ident[:])
         x_words = x_sb[:].bitcast(F32).rearrange("p bb (w j) -> p bb j w", j=2)
-        x_t = psum_t.tile([P, 2, B], F32, tag="h_t")
+        x_t = psum_t.tile([P, 2, B], F32, name="h_t")
         for bb in range(B_BLOCKS):
             for j in range(2):
                 nc.tensor.transpose(
@@ -222,10 +204,23 @@ def tile_plelayer_pa_kernel(
             scales=x_scales[:],
             in_=x_grouped[:].rearrange("p b t -> p (b t)"),
         )
-        bias_f = const.tile([P, SETS, U_BLOCKS, E], F32)
-        nc.gpsimd.tensor_copy(out=bias_f[:], in_=bias_bf[:])
 
-        mixer = const.tile([P, N_GROUPS, O_SLOTS, GB], F32)
+        ident_bf = const.tile([P, P], BF16)
+        make_identity(nc, ident_bf[:])
+        bias_t = psum_t.tile([P, E, P], BF16, name="h_t")
+        for e in range(E):
+            nc.tensor.transpose(
+                out=bias_t[:, e, :],
+                in_=bias_rows[:].rearrange("r (p e) -> r e p", e=E)[:, e, :],
+                identity=ident_bf[:],
+            )
+        bias_f = const.tile([P, SETS, U_BLOCKS, E], F32)
+        nc.scalar.copy(
+            out=bias_f[:].rearrange("p s ub e -> p (s ub) e"),
+            in_=bias_t[:, :, 0 : SETS * U_BLOCKS].rearrange("p e r -> p r e"),
+        )
+
+        mixer = const.tile([P, N_ROWGROUPS, O_SLOTS, GB], F32)
         nc.gpsimd.memset(mixer[:], 0.0)
 
         def make_mixer():
@@ -247,7 +242,7 @@ def tile_plelayer_pa_kernel(
                     in1=own_row[:].unsqueeze(1).to_broadcast([P, SETS * E, GB]),
                     op=ALU.mult,
                 )
-            per_block = N_GROUPS // B_BLOCKS
+            per_block = N_ROWGROUPS // B_BLOCKS
             for bb in range(B_BLOCKS):
                 turned = psum_t.tile([P, T, P], F32, name="h_t")
                 for o in range(T):
@@ -276,19 +271,13 @@ def tile_plelayer_pa_kernel(
         for o in range(SETS):
             for bb in range(B_BLOCKS):
                 terms[(o, bb)] = 0 if (o, bb) == (0, 0) else 1
-        hidden_s = []
-        for ub in range(U_BLOCKS):
-            block = gated_pool.tile([P, N_GROUPS, E, GB], F32, name="gated")
-            hidden_s.append(block)
+        hidden_s = [const.tile([P, N_ROWGROUPS, E, GB], F32, name="hidden_s_%d" % ub) for ub in range(U_BLOCKS)]
         products = {}
         hidden = {}
         hidden_t = {}
-        acc = psum_acc.tile([P, U], F32, name="acc")
         gated_tiles = {}
-        last_gated = N_TASK_EXPERTS - DIRECT - 1
-
-        def is_direct(n):
-            return n > last_gated or n % SPATH_EVERY != 0
+        acc = psum_acc.tile([P, U], F32, name="acc")
+        last_gated = N_TASK_EXPERTS - 2
 
         def multiply(s, e):
             eg, i = divmod(e, E_GROUP)
@@ -325,45 +314,42 @@ def tile_plelayer_pa_kernel(
                 )
 
         def transpose(n, bb):
-            s, e = experts[n]
             h_t = psum_t.tile([P, U], F32, name="h_t")
             for ub in range(U_BLOCKS):
                 nc.tensor.transpose(
                     out=h_t[:, ub * P : (ub + 1) * P],
-                    in_=hidden[(s, e)][:, ub, bb * P : (bb + 1) * P],
+                    in_=hidden[experts[n]][:, ub, bb * P : (bb + 1) * P],
                     identity=ident[:],
                 )
             hidden_t[(n, bb)] = h_t
 
         def add_term(o, bb, source, gate):
-            if terms.get((o, bb), 0) == 0:
+            if terms[(o, bb)] == 0:
                 nc.vector.tensor_scalar_mul(out=sums[o][:, bb, :], in0=source, scalar1=gate)
             else:
                 nc.vector.scalar_tensor_tensor(
                     out=sums[o][:, bb, :], in0=source, scalar=gate, in1=sums[o][:, bb, :], op0=ALU.mult, op1=ALU.add
                 )
-            terms[(o, bb)] = terms.get((o, bb), 0) + 1
+            terms[(o, bb)] += 1
 
         def on_vector(n, bb):
             s, e = experts[n]
             col = (s - 1) * G_TASK + e
             add_term(s - 1, bb, hidden_t[(n, bb)][:], g_task[:, bb, col : col + 1])
-            if is_direct(n) or bb == 1:
+            if n > last_gated or bb == 1:
                 col = (s - 1) * E + e
                 add_term(T, bb, hidden_t[(n, bb)][:], g_share[:, bb, col : col + 1])
 
-        def on_scalar(n, bb):
+        def on_scalar(n):
             s, e = experts[n]
             col = (s - 1) * E + e
             gated_tiles[n] = gated_pool.tile([P, U], F32, name="gated")
             nc.scalar.activation(
                 out=gated_tiles[n][:],
-                in_=hidden_t[(n, bb)][:],
+                in_=hidden_t[(n, 0)][:],
                 func=ACT.Copy,
-                scale=g_share[:, bb, col : col + 1],
+                scale=g_share[:, 0, col : col + 1],
             )
-
-        last_added = max(n for n in range(last_gated + 1) if not is_direct(n))
 
         def add_transposed(n):
             for ub in range(U_BLOCKS):
@@ -372,7 +358,7 @@ def tile_plelayer_pa_kernel(
                     lhsT=gated_tiles[n][:, ub * P : (ub + 1) * P],
                     rhs=ident[:],
                     start=(n == 0 and ub == 0),
-                    stop=(n == last_added and ub == U_BLOCKS - 1),
+                    stop=(n == last_gated and ub == U_BLOCKS - 1),
                     is_transpose=True,
                 )
 
@@ -386,14 +372,13 @@ def tile_plelayer_pa_kernel(
                 )
             nc.vector.tensor_tensor(out=sums[T][:, 0, :], in0=back[:], in1=sums[T][:, 0, :], op=ALU.add)
 
-        def finish(o):
-            for bb in range(B_BLOCKS):
-                if (o, bb) == (0, 0):
-                    nc.vector.tensor_tensor(
-                        out=sums[o][:, bb, :], in0=sums[o][:, bb, :], in1=late_part[:], op=ALU.add
-                    )
-                target = out_0[o] if o < T else out_1
-                nc.sync.dma_start(out=target[bb * P : (bb + 1) * P, :], in_=sums[o][:, bb, :])
+        def finish(o, bb):
+            if (o, bb) == (0, 0):
+                nc.vector.tensor_tensor(
+                    out=sums[o][:, bb, :], in0=sums[o][:, bb, :], in1=late_part[:], op=ALU.add
+                )
+            target = out_0[o] if o < T else out_1
+            nc.sync.dma_start(out=target[bb * P : (bb + 1) * P, :], in_=sums[o][:, bb, :])
 
         group_rows = {}
         group_parts = {}
@@ -407,32 +392,24 @@ def tile_plelayer_pa_kernel(
                     in_=hidden_s[ub][:, g].rearrange("p e c -> p (e c)"),
                     identity=ident[:],
                 )
-            rows = rows_pool.tile([P, U], F32, name="rows")
-            if g % ROWS_V == ROWS_V - 1:
-                nc.vector.tensor_copy(out=rows[:], in_=turned_g[:])
-            else:
-                nc.scalar.copy(out=rows[:], in_=turned_g[:])
-            group_rows[g] = rows
+            group_rows[g] = rows_pool.tile([P, U], F32, name="rows")
+            nc.scalar.copy(out=group_rows[g][:], in_=turned_g[:])
 
         def group_mix(g):
-            mixed = psum_t.tile([P, U], F32, name="h_t")
+            group_parts[g] = psum_t.tile([P, U], F32, name="h_t")
             nc.tensor.matmul(
-                out=mixed[:],
+                out=group_parts[g][:],
                 lhsT=mixer[:, g].rearrange("p o c -> p (o c)"),
                 rhs=group_rows[g][:],
                 start=True,
                 stop=True,
             )
-            group_parts[g] = mixed
 
         def group_out(g):
             quad, place = divmod(g, QUAD)
             if place == 0:
                 part_tiles[quad] = part_pool.tile([P, QUAD, U], F32, name="part")
-            if g % PART_V == PART_V - 1:
-                nc.vector.tensor_copy(out=part_tiles[quad][:, place, :], in_=group_parts[g][:])
-            else:
-                nc.scalar.copy(out=part_tiles[quad][:, place, :], in_=group_parts[g][:])
+            nc.scalar.copy(out=part_tiles[quad][:, place, :], in_=group_parts[g][:])
             if place == QUAD - 1:
                 rows = slice(quad * QUAD * GB, (quad + 1) * QUAD * GB)
                 for o in range(SETS):
@@ -441,78 +418,81 @@ def tile_plelayer_pa_kernel(
                         out=target[rows, :].rearrange("(q c) u -> c q u", c=GB),
                         in_=part_tiles[quad][o * GB : (o + 1) * GB, :, :],
                     )
-            if g % (N_GROUPS // B_BLOCKS) == N_GROUPS // B_BLOCKS - 1:
-                bb = g // (N_GROUPS // B_BLOCKS)
+            bb, place = divmod(g, N_ROWGROUPS // B_BLOCKS)
+            if place == N_ROWGROUPS // B_BLOCKS - 1:
                 for o in range(SETS):
                     source = out_0[o] if o < T else out_1
                     target = late_part[:] if (o, bb) == (0, 0) else sums[o][:, bb, :]
                     nc.sync.dma_start(out=target, in_=source[bb * P : (bb + 1) * P, :])
 
-        units = [(s, eg, ub) for s in range(1, SETS) for eg in range(GROUPS) for ub in range(U_BLOCKS)]
-        made = {"count": 0, "piece": 0}
-
-        def next_unit(engine, hold=False):
-            regroup(*units[made["count"]], engine, 0, 1, hold)
-            if made["count"] > 0:
-                quantise(*units[made["count"] - 1])
-            made["count"] += 1
-
         for ub in range(U_BLOCKS):
             pieces = 2 if ub == 0 else 1
+            width = P // pieces
             for piece in range(pieces):
-                regroup(0, 0, ub, "V", piece, pieces)
-                regroup(0, 1, ub, "S", piece, pieces)
+                regroup((0, 0, ub), "V", piece * width, (piece + 1) * width)
+                regroup((0, 1, ub), "S", piece * width, (piece + 1) * width)
             if ub > 0:
-                quantise(0, 1, ub - 1)
-            quantise(0, 0, ub)
-        quantise(0, 1, U_BLOCKS - 1)
+                quantise((0, 1, ub - 1))
+            quantise((0, 0, ub))
+        quantise((0, 1, U_BLOCKS - 1))
+
+        def next_unit(k):
+            regroup(units[k], "V", 0, P, k == AHEAD - 1)
+            if k > 0:
+                quantise(units[k - 1])
+
         for e in range(E):
             multiply(0, e)
             bias_relu(0, e)
-            if e < U_BLOCKS:
-                next_unit("V")
+            if e < RELU_UNITS:
+                next_unit(e)
         make_mixer()
 
-        order = list(range(N_GROUPS // B_BLOCKS, N_GROUPS)) + list(range(N_GROUPS // B_BLOCKS))
+        order = list(range(N_ROWGROUPS // 2, N_ROWGROUPS)) + list(range(N_ROWGROUPS // 2))
+        rest = AHEAD - RELU_UNITS
         group_turn(order[0])
-        for g in range(N_GROUPS):
-            if g + 1 < N_GROUPS:
-                group_turn(order[g + 1])
-            group_mix(order[g])
-            group_out(order[g])
-            if g % AHEAD_EVERY != AHEAD_EVERY - 1:
-                next_unit("V", g == N_GROUPS - 1 - (1 if (N_GROUPS - 1) % AHEAD_EVERY == AHEAD_EVERY - 1 else 0))
+        for j in range(N_ROWGROUPS):
+            if j + 1 < N_ROWGROUPS:
+                group_turn(order[j + 1])
+            group_mix(order[j])
+            group_out(order[j])
+            for k in range(j * rest // N_ROWGROUPS, (j + 1) * rest // N_ROWGROUPS):
+                next_unit(RELU_UNITS + k)
+        quantise(units[AHEAD - 1])
 
-        quantise(*units[made["count"] - 1])
-
-        finished = []
-        if MANUAL:
-            ctx.enter_context(tc.manual_schedule())
+        g_units = len(units) - AHEAD
+        quant_steps = [Q_FIRST + (Q_LAST - Q_FIRST) * j // (g_units - 1) for j in range(g_units)]
+        ctx.enter_context(tc.manual_schedule())
         for i in range(N_TASK_EXPERTS + ADD_LAG + 1):
-            if i % G_STEPS == 0:
-                if made["piece"] == 1:
-                    quantise(*units[made["count"]])
-                    made["count"] += 1
-                    made["piece"] = 0
-                if made["count"] < len(units):
-                    for piece in range(G_PIECES):
-                        regroup(*units[made["count"]], "G", piece, G_PIECES)
-                    made["piece"] = 1
+            started = None
+            if i == 0:
+                started = AHEAD
+            elif i in quant_steps:
+                done = AHEAD + quant_steps.index(i)
+                quantise(units[done])
+                if done + 1 < len(units):
+                    started = done + 1
+            if started is not None:
+                regroup(units[started], "G", 0, G_CUT, True)
             if 2 <= i < N_TASK_EXPERTS + 2:
-                if not is_direct(i - 2):
-                    on_scalar(i - 2, 0)
+                if i - 2 <= last_gated:
+                    on_scalar(i - 2)
                 on_vector(i - 2, 1)
                 on_vector(i - 2, 0)
             if i < N_TASK_EXPERTS:
                 multiply(*experts[i])
                 bias_relu(*experts[i])
+            if started is not None:
+                regroup(units[started], "S", G_CUT, P)
             if 1 <= i <= N_TASK_EXPERTS:
                 transpose(i - 1, 0)
                 transpose(i - 1, 1)
-            if ADD_LAG <= i and i - ADD_LAG <= last_gated and not is_direct(i - ADD_LAG):
+            if ADD_LAG <= i <= last_gated + ADD_LAG:
                 add_transposed(i - ADD_LAG)
-            if i - ADD_LAG == last_gated:
+            if i == last_gated + ADD_LAG:
                 turn_back()
             if i >= 2 and (i - 2) % E == E - 1:
-                finish((i - 2) // E)
-        finish(T)
+                for bb in range(B_BLOCKS):
+                    finish((i - 2) // E, bb)
+        for bb in range(B_BLOCKS):
+            finish(T, bb)

@@ -32,10 +32,39 @@ QUAD = 4
 RAW_BUFS = 6
 RELU_UNITS = 4
 AHEAD = 19
-G_CUT = 112
+G_CUT = 128
 Q_FIRST = 3
 Q_LAST = 27
 ADD_LAG = 3
+LEAD_AT = ()
+FIRST_I = 0
+S_PRE = 128
+PARTS_MX = 0
+PAIR = 1
+SPLIT = 0
+BY_CHUNK = 2
+HT5 = 0
+QSTEP = 0
+SH_ENG = ("S", "S", "S", "S")
+UB_ORDER = 0
+DIRECT_MOD = 1000
+A_FIRST = 1
+GATE_LATE = 0
+T_ORDER = (0, 1)
+MIX_AT = 7
+GADD = 0
+GADD_FIRST = 1
+TAIL_BUFS = 6
+T_FIRST = 0
+LATE_GROUPS = 0
+LATE_FROM = 0
+LATE_EVERY = 3
+LATE_PIECES = 1
+LATE_1 = ()
+LATE_MIX = 1
+LATE_OUT = 2
+LATE_O = 1
+FINISH_LATE = 28
 
 FLOPS = 2 * B * D * U * E * SETS
 
@@ -50,13 +79,14 @@ def tile_plelayer_pa_kernel(
         const = ctx.enter_context(tc.tile_pool(name="const", bufs=1))
         raw_pool = ctx.enter_context(tc.tile_pool(name="raw", bufs=RAW_BUFS))
         unit_pool = ctx.enter_context(tc.tile_pool(name="unit", bufs=3))
-        held_pool = ctx.enter_context(tc.tile_pool(name="held", bufs=1))
+        held_pool = ctx.enter_context(tc.tile_pool(name="held", bufs=PAIR))
         codes_pool = ctx.enter_context(tc.tile_pool(name="codes", bufs=5))
         h_pool = ctx.enter_context(tc.tile_pool(name="h", bufs=3))
         rows_pool = ctx.enter_context(tc.tile_pool(name="rows", bufs=2))
         part_pool = ctx.enter_context(tc.tile_pool(name="part", bufs=2))
         gated_pool = ctx.enter_context(tc.tile_pool(name="gated", bufs=2))
-        psum_mx = ctx.enter_context(tc.psum_pool(name="psum_mx", bufs=3))
+        tail_pool = ctx.enter_context(tc.tile_pool(name="tail", bufs=TAIL_BUFS))
+        psum_mx = ctx.enter_context(tc.psum_pool(name="psum_mx", bufs=2 if SPLIT or HT5 else 3))
         psum_t = ctx.enter_context(tc.psum_pool(name="psum_t", bufs=4))
         psum_acc = ctx.enter_context(tc.psum_pool(name="psum_acc", bufs=1))
 
@@ -87,8 +117,8 @@ def tile_plelayer_pa_kernel(
         unit_tiles = {}
         readers = {}
         loads = [(s, ub) for s in range(SETS) for ub in range(U_BLOCKS)]
-        units = [(s, eg, ub) for s in (1, 2) for ub in range(U_BLOCKS) for eg in range(GROUPS)]
-        units += [(s, eg, ub) for s in range(3, SETS) for eg in range(GROUPS) for ub in range(U_BLOCKS)]
+        units = [(s, eg, ub) for s in range(1, 1 + BY_CHUNK) for ub in range(U_BLOCKS) for eg in range(GROUPS)]
+        units += [(s, eg, ub) for s in range(1 + BY_CHUNK, SETS) for eg in range(GROUPS) for ub in range(U_BLOCKS)]
 
         def load_next(pieces=1):
             if loads:
@@ -266,17 +296,21 @@ def tile_plelayer_pa_kernel(
 
         experts = [(1 + t, e) for t in range(T) for e in range(E)]
         sums = [const.tile([P, B_BLOCKS, U], F32, name="sum_%d" % o) for o in range(SETS)]
-        late_part = const.tile([P, U], F32)
+        late_part = {(o, 0): const.tile([P, U], F32, name="late_part_%d" % o) for o in range(LATE_O)}
+        for o in LATE_1:
+            late_part[(o, 1)] = const.tile([P, U], F32, name="late_1_%d" % o)
+        tail = const.tile([P, max(GADD, 1)], F32)
         terms = {}
         for o in range(SETS):
             for bb in range(B_BLOCKS):
-                terms[(o, bb)] = 0 if (o, bb) == (0, 0) else 1
+                terms[(o, bb)] = 0 if (o, bb) in late_part else 1
         hidden_s = [const.tile([P, N_ROWGROUPS, E, GB], F32, name="hidden_s_%d" % ub) for ub in range(U_BLOCKS)]
         products = {}
         hidden = {}
         hidden_t = {}
         gated_tiles = {}
         acc = psum_acc.tile([P, U], F32, name="acc")
+        acc2 = []
         last_gated = N_TASK_EXPERTS - 2
 
         def multiply(s, e):
@@ -284,7 +318,10 @@ def tile_plelayer_pa_kernel(
             codes, scales = code_tiles[(s, eg)]
             products[(s, e)] = []
             for half in range(U_BLOCKS // 2):
-                product = psum_mx.tile([P, 2, B], F32, name="product")
+                if (SPLIT or HT5) and s == 0 and len(products) % 3 == 2 and half == 0:
+                    product = psum_acc.tile([P, 2, B], F32, name="spare")
+                else:
+                    product = psum_mx.tile([P, 2, B], F32, name="product")
                 for j in range(2):
                     ub = 2 * half + j
                     cols = slice(ub * UNIT_WORDS + i * P, ub * UNIT_WORDS + (i + 1) * P)
@@ -314,7 +351,10 @@ def tile_plelayer_pa_kernel(
                 )
 
         def transpose(n, bb):
-            h_t = psum_t.tile([P, U], F32, name="h_t")
+            if HT5 and (2 * n + (bb if T_FIRST == 0 else 1 - bb)) % 5 == 4:
+                h_t = psum_acc.tile([P, U], F32, name="spare")
+            else:
+                h_t = psum_t.tile([P, U], F32, name="h_t")
             for ub in range(U_BLOCKS):
                 nc.tensor.transpose(
                     out=h_t[:, ub * P : (ub + 1) * P],
@@ -323,26 +363,46 @@ def tile_plelayer_pa_kernel(
                 )
             hidden_t[(n, bb)] = h_t
 
-        def add_term(o, bb, source, gate):
+        def add_term(o, bb, source, gate, keep=U):
             if terms[(o, bb)] == 0:
-                nc.vector.tensor_scalar_mul(out=sums[o][:, bb, :], in0=source, scalar1=gate)
+                nc.vector.tensor_scalar_mul(out=sums[o][:, bb, 0:keep], in0=source, scalar1=gate)
             else:
                 nc.vector.scalar_tensor_tensor(
-                    out=sums[o][:, bb, :], in0=source, scalar=gate, in1=sums[o][:, bb, :], op0=ALU.mult, op1=ALU.add
+                    out=sums[o][:, bb, 0:keep], in0=source, scalar=gate, in1=sums[o][:, bb, 0:keep], op0=ALU.mult, op1=ALU.add
                 )
             terms[(o, bb)] += 1
 
-        def on_vector(n, bb):
+        def on_vector(n, bb, which):
             s, e = experts[n]
             col = (s - 1) * G_TASK + e
-            add_term(s - 1, bb, hidden_t[(n, bb)][:], g_task[:, bb, col : col + 1])
-            if n > last_gated or bb == 1:
+            if which == 0:
+                add_term(s - 1, bb, hidden_t[(n, bb)][:], g_task[:, bb, col : col + 1])
+            elif n > last_gated or bb == 1 or n % DIRECT_MOD == DIRECT_MOD - 1:
                 col = (s - 1) * E + e
-                add_term(T, bb, hidden_t[(n, bb)][:], g_share[:, bb, col : col + 1])
+                keep = U if n > last_gated else U - SPLIT * P
+                if GADD and bb == 1:
+                    keep = U - GADD
+                add_term(T, bb, hidden_t[(n, bb)][:, 0:keep], g_share[:, bb, col : col + 1], keep)
+
+        def gate_tail(n):
+            s, e = experts[n]
+            col = (s - 1) * E + e
+            tile = tail_pool.tile([P, GADD], F32, name="gated_g")
+            nc.scalar.activation(
+                out=tile[:],
+                in_=hidden_t[(n, 1)][:, U - GADD : U],
+                func=ACT.Copy,
+                scale=g_share[:, 1, col : col + 1],
+            )
+            nc.gpsimd.tensor_tensor(out=tail[:], in0=tile[:], in1=tail[:], op=ALU.add)
 
         def on_scalar(n):
             s, e = experts[n]
             col = (s - 1) * E + e
+            if GADD and GADD_FIRST:
+                gate_tail(n)
+            if n > last_gated or n % DIRECT_MOD == DIRECT_MOD - 1:
+                return
             gated_tiles[n] = gated_pool.tile([P, U], F32, name="gated")
             nc.scalar.activation(
                 out=gated_tiles[n][:],
@@ -350,6 +410,14 @@ def tile_plelayer_pa_kernel(
                 func=ACT.Copy,
                 scale=g_share[:, 0, col : col + 1],
             )
+            if SPLIT:
+                gated_tiles[(n, 1)] = gated_pool.tile([P, SPLIT * P], F32, name="gated_1")
+                nc.scalar.activation(
+                    out=gated_tiles[(n, 1)][:],
+                    in_=hidden_t[(n, 1)][:, U - SPLIT * P : U],
+                    func=ACT.Copy,
+                    scale=g_share[:, 1, col : col + 1],
+                )
 
         def add_transposed(n):
             for ub in range(U_BLOCKS):
@@ -362,7 +430,31 @@ def tile_plelayer_pa_kernel(
                     is_transpose=True,
                 )
 
+            if SPLIT:
+                if n == 0:
+                    acc2.append(psum_acc.tile([P, SPLIT * P], F32, name="spare"))
+                for j in range(SPLIT):
+                    nc.tensor.matmul(
+                        out=acc2[0][:, j * P : (j + 1) * P],
+                        lhsT=gated_tiles[(n, 1)][:, j * P : (j + 1) * P],
+                        rhs=ident[:],
+                        start=(n == 0 and j == 0),
+                        stop=(n == last_gated and j == SPLIT - 1),
+                        is_transpose=True,
+                    )
+
         def turn_back():
+            if SPLIT:
+                acc2_sb = gated_pool.tile([P, SPLIT * P], F32, name="gated_1")
+                nc.scalar.copy(out=acc2_sb[:], in_=acc2[0][:])
+                back2 = psum_t.tile([P, SPLIT * P], F32, name="h_t")
+                for j in range(SPLIT):
+                    nc.tensor.transpose(
+                        out=back2[:, j * P : (j + 1) * P], in_=acc2_sb[:, j * P : (j + 1) * P], identity=ident[:]
+                    )
+                nc.vector.tensor_tensor(
+                    out=sums[T][:, 1, U - SPLIT * P : U], in0=back2[:], in1=sums[T][:, 1, U - SPLIT * P : U], op=ALU.add
+                )
             acc_sb = gated_pool.tile([P, U], F32, name="gated")
             nc.scalar.copy(out=acc_sb[:], in_=acc[:])
             back = psum_t.tile([P, U], F32, name="h_t")
@@ -373,12 +465,16 @@ def tile_plelayer_pa_kernel(
             nc.vector.tensor_tensor(out=sums[T][:, 0, :], in0=back[:], in1=sums[T][:, 0, :], op=ALU.add)
 
         def finish(o, bb):
-            if (o, bb) == (0, 0):
+            if (o, bb) in late_part:
                 nc.vector.tensor_tensor(
-                    out=sums[o][:, bb, :], in0=sums[o][:, bb, :], in1=late_part[:], op=ALU.add
+                    out=sums[o][:, bb, :], in0=sums[o][:, bb, :], in1=late_part[(o, bb)][:], op=ALU.add
                 )
             target = out_0[o] if o < T else out_1
-            nc.sync.dma_start(out=target[bb * P : (bb + 1) * P, :], in_=sums[o][:, bb, :])
+            if GADD and (o, bb) == (T, 1):
+                nc.sync.dma_start(out=target[bb * P : (bb + 1) * P, U - GADD : U], in_=tail[:])
+                nc.sync.dma_start(out=target[bb * P : (bb + 1) * P, 0 : U - GADD], in_=sums[o][:, bb, 0 : U - GADD])
+            else:
+                nc.sync.dma_start(out=target[bb * P : (bb + 1) * P, :], in_=sums[o][:, bb, :])
 
         group_rows = {}
         group_parts = {}
@@ -395,12 +491,17 @@ def tile_plelayer_pa_kernel(
             group_rows[g] = rows_pool.tile([P, U], F32, name="rows")
             nc.scalar.copy(out=group_rows[g][:], in_=turned_g[:])
 
-        def group_mix(g):
-            group_parts[g] = psum_t.tile([P, U], F32, name="h_t")
+        def group_mix(g, piece=0, pieces=1):
+            if piece == 0:
+                if PARTS_MX:
+                    group_parts[g] = psum_mx.tile([P, U], F32, name="product")
+                else:
+                    group_parts[g] = psum_t.tile([P, U], F32, name="h_t")
+            cols = slice(piece * U // pieces, (piece + 1) * U // pieces)
             nc.tensor.matmul(
-                out=group_parts[g][:],
+                out=group_parts[g][:, cols],
                 lhsT=mixer[:, g].rearrange("p o c -> p (o c)"),
-                rhs=group_rows[g][:],
+                rhs=group_rows[g][:, cols],
                 start=True,
                 stop=True,
             )
@@ -422,77 +523,179 @@ def tile_plelayer_pa_kernel(
             if place == N_ROWGROUPS // B_BLOCKS - 1:
                 for o in range(SETS):
                     source = out_0[o] if o < T else out_1
-                    target = late_part[:] if (o, bb) == (0, 0) else sums[o][:, bb, :]
+                    target = late_part[(o, bb)][:] if (o, bb) in late_part else sums[o][:, bb, :]
                     nc.sync.dma_start(out=target, in_=source[bb * P : (bb + 1) * P, :])
+                    if GADD and (o, bb) == (T, 1):
+                        nc.sync.dma_start(out=tail[:], in_=source[bb * P : (bb + 1) * P, U - GADD : U])
 
         for ub in range(U_BLOCKS):
             pieces = 2 if ub == 0 else 1
             width = P // pieces
             for piece in range(pieces):
                 regroup((0, 0, ub), "V", piece * width, (piece + 1) * width)
-                regroup((0, 1, ub), "S", piece * width, (piece + 1) * width)
+                regroup((0, 1, ub), SH_ENG[ub], piece * width, (piece + 1) * width)
             if ub > 0:
                 quantise((0, 1, ub - 1))
             quantise((0, 0, ub))
         quantise((0, 1, U_BLOCKS - 1))
 
         def next_unit(k):
-            regroup(units[k], "V", 0, P, k == AHEAD - 1)
+            if S_PRE < P and k >= RELU_UNITS:
+                regroup(units[k], "V", 0, S_PRE, k == AHEAD - 1)
+                regroup(units[k], "S", S_PRE, P)
+            else:
+                regroup(units[k], "V", 0, P, k == AHEAD - 1)
             if k > 0:
                 quantise(units[k - 1])
 
-        for e in range(E):
-            multiply(0, e)
-            bias_relu(0, e)
-            if e < RELU_UNITS:
-                next_unit(e)
-        make_mixer()
+        if MIX_AT < 0:
+            make_mixer()
+        if UB_ORDER:
+            count = 0
+            for ub in range(U_BLOCKS):
+                for eg in range(GROUPS):
+                    codes, scales = code_tiles[(0, eg)]
+                    for pair in range(2):
+                        if (SPLIT or HT5) and count % 3 == 2:
+                            product = psum_acc.tile([P, 2, B], F32, name="spare")
+                        else:
+                            product = psum_mx.tile([P, 2, B], F32, name="product")
+                        count += 1
+                        for j in range(2):
+                            i = 2 * pair + j
+                            cols = slice(ub * UNIT_WORDS + i * P, ub * UNIT_WORDS + (i + 1) * P)
+                            nc.tensor.matmul_mx(
+                                out=product[:, j, :],
+                                lhsT=codes[:, cols].bitcast(FP8X4),
+                                lhsT_scale=scales[:, cols],
+                                rhs=x_codes[:].bitcast(FP8X4),
+                                rhs_scale=x_scales[:],
+                                start=True,
+                                stop=True,
+                            )
+                        for j in range(2):
+                            e = eg * E_GROUP + 2 * pair + j
+                            nc.scalar.activation(
+                                out=hidden_s[ub][:, :, e, :],
+                                in_=product[:, j, :].rearrange("p (g c) -> p g c", c=GB),
+                                func=ACT.Relu,
+                                bias=bias_f[:, 0, ub, e : e + 1],
+                                scale=1.0,
+                            )
+                if ub < RELU_UNITS:
+                    next_unit(ub)
+                if ub == MIX_AT:
+                    make_mixer()
+        else:
+            for e in range(E):
+                multiply(0, e)
+                bias_relu(0, e)
+                if e < RELU_UNITS:
+                    next_unit(e)
+                if e == MIX_AT:
+                    make_mixer()
 
         order = list(range(N_ROWGROUPS // 2, N_ROWGROUPS)) + list(range(N_ROWGROUPS // 2))
         rest = AHEAD - RELU_UNITS
+        early = order[: N_ROWGROUPS - LATE_GROUPS]
+        late = order[N_ROWGROUPS - LATE_GROUPS :]
         group_turn(order[0])
-        for j in range(N_ROWGROUPS):
-            if j + 1 < N_ROWGROUPS:
+        for j in range(len(early)):
+            if j + 1 < len(early):
                 group_turn(order[j + 1])
             group_mix(order[j])
             group_out(order[j])
-            for k in range(j * rest // N_ROWGROUPS, (j + 1) * rest // N_ROWGROUPS):
+            if j in LEAD_AT:
+                n = LEAD_AT.index(j)
+                multiply(*experts[n])
+                bias_relu(*experts[n])
+            for k in range(j * rest // len(early), (j + 1) * rest // len(early)):
                 next_unit(RELU_UNITS + k)
         quantise(units[AHEAD - 1])
 
         g_units = len(units) - AHEAD
-        quant_steps = [Q_FIRST + (Q_LAST - Q_FIRST) * j // (g_units - 1) for j in range(g_units)]
+        if PAIR > 1:
+            batches = [list(range(k, min(k + PAIR, len(units)))) for k in range(AHEAD, len(units), PAIR)]
+        else:
+            batches = [[k] for k in range(AHEAD, len(units))]
+        g_batches = len(batches)
+        quant_steps = [Q_FIRST + (Q_LAST - Q_FIRST) * j // (g_batches - 1) for j in range(g_batches)]
         ctx.enter_context(tc.manual_schedule())
-        for i in range(N_TASK_EXPERTS + ADD_LAG + 1):
-            started = None
-            if i == 0:
-                started = AHEAD
-            elif i in quant_steps:
-                done = AHEAD + quant_steps.index(i)
-                quantise(units[done])
-                if done + 1 < len(units):
-                    started = done + 1
-            if started is not None:
-                regroup(units[started], "G", 0, G_CUT, True)
+        todo = []
+        qpos = quant_steps if QSTEP == 0 else [Q_FIRST * 3 + QSTEP * j for j in range(g_batches)]
+        if QSTEP == 0:
+            qpos = [3 * q for q in quant_steps]
+
+        def slot(place):
+            if place in qpos:
+                j = qpos.index(place)
+                for k in batches[j]:
+                    quantise(units[k])
+                if j + 1 < g_batches:
+                    for k in batches[j + 1]:
+                        regroup(units[k], "G", 0, G_CUT, True)
+                    todo.extend(batches[j + 1])
+
+        for i in range(FIRST_I, N_TASK_EXPERTS + ADD_LAG + 1):
+            if i == FIRST_I:
+                for k in batches[0]:
+                    regroup(units[k], "G", 0, G_CUT, True)
+                todo += batches[0]
+            slot(3 * i)
             if 2 <= i < N_TASK_EXPERTS + 2:
-                if i - 2 <= last_gated:
+                if (i - 2 <= last_gated or GADD) and not GATE_LATE:
                     on_scalar(i - 2)
-                on_vector(i - 2, 1)
-                on_vector(i - 2, 0)
-            if i < N_TASK_EXPERTS:
+                on_vector(i - 2, 1, 0)
+                slot(3 * i + 1)
+                on_vector(i - 2, 1, 1)
+                slot(3 * i + 2)
+                on_vector(i - 2, 0, 0)
+                on_vector(i - 2, 0, 1)
+            else:
+                slot(3 * i + 1)
+                slot(3 * i + 2)
+            if len(LEAD_AT) <= i < N_TASK_EXPERTS:
                 multiply(*experts[i])
                 bias_relu(*experts[i])
-            if started is not None:
-                regroup(units[started], "S", G_CUT, P)
-            if 1 <= i <= N_TASK_EXPERTS:
-                transpose(i - 1, 0)
-                transpose(i - 1, 1)
-            if ADD_LAG <= i <= last_gated + ADD_LAG:
+            if GATE_LATE and 2 <= i <= last_gated + 2:
+                on_scalar(i - 2)
+            if todo and G_CUT < P:
+                regroup(units[todo.pop(0)], "S", G_CUT, P)
+            if A_FIRST and ADD_LAG <= i <= last_gated + ADD_LAG:
                 add_transposed(i - ADD_LAG)
+            for bb in T_ORDER:
+                if 1 <= i <= N_TASK_EXPERTS:
+                    transpose(i - 1, bb)
+                if late and LATE_PIECES == 4 and i >= LATE_FROM:
+                    j, place = divmod(i - LATE_FROM, LATE_EVERY)
+                    if place in (LATE_MIX, LATE_MIX + 1) and j < len(late):
+                        group_mix(late[j], 2 * (place - LATE_MIX) + bb, 4)
+            if not A_FIRST and ADD_LAG <= i <= last_gated + ADD_LAG and (i - ADD_LAG) % DIRECT_MOD != DIRECT_MOD - 1:
+                add_transposed(i - ADD_LAG)
+            if late and i >= LATE_FROM:
+                j, place = divmod(i - LATE_FROM, LATE_EVERY)
+                if place == 0 and j < len(late):
+                    group_turn(late[j])
+                if LATE_PIECES == 1 and place == LATE_MIX and j < len(late):
+                    group_mix(late[j])
+                if LATE_PIECES == 2 and place in (LATE_MIX, LATE_MIX + 1) and j < len(late):
+                    group_mix(late[j], place - LATE_MIX, 2)
+                jj = j - LATE_OUT // LATE_EVERY
+                if place == LATE_OUT % LATE_EVERY and 0 <= jj < len(late):
+                    group_out(late[jj])
             if i == last_gated + ADD_LAG:
                 turn_back()
             if i >= 2 and (i - 2) % E == E - 1:
-                for bb in range(B_BLOCKS):
-                    finish((i - 2) // E, bb)
+                o = (i - 2) // E
+                if i < N_TASK_EXPERTS + 1:
+                    finish(o, 1)
+                else:
+                    finish(o, 1)
+                if not late or (o, 0) not in late_part or i >= FINISH_LATE:
+                    finish(o, 0)
+            if late and i == FINISH_LATE:
+                for o in range(LATE_O):
+                    if o * E + E - 1 + 2 < FINISH_LATE:
+                        finish(o, 0)
         for bb in range(B_BLOCKS):
             finish(T, bb)

from contextlib import ExitStack

import concourse.mybir as mybir
from concourse.masks import make_identity

F32 = mybir.dt.float32
BF16 = mybir.dt.bfloat16
U32 = mybir.dt.uint32
U8 = mybir.dt.uint8
FP8X4 = mybir.dt.float8_e4m3fn_x4
ALU = mybir.AluOpType
ACT = mybir.ActivationFunctionType
AXIS_X = mybir.AxisListType.X

P = 128
PACK = 4
T, B, D, U, E = 4, 256, 512, 512, 8
SETS = T + 1
B_BLOCKS = B // P
U_BLOCKS = U // P
E_GROUP = 4
GROUPS = E // E_GROUP
UNIT_WORDS = E_GROUP * P
CHUNK = P * E
G_TASK = 2 * E
G_SHARE = SETS * E
N_TASK_EXPERTS = T * E
GB = 16
N_ROWGROUPS = B // GB
O_SLOTS = P // GB
QUAD = 4
RAW_BUFS = 6
RELU_UNITS = 4
AHEAD = 19
G_CUT = 128
Q_FIRST = 3
Q_LAST = 27
ADD_LAG = 3
LEAD_AT = ()
FIRST_I = 0
S_PRE = 128
PARTS_MX = 0
PAIR = 1
SPLIT = 0
BY_CHUNK = 2
HT5 = 0
QSTEP = 0
SH_ENG = ("S", "S", "S", "S")
UB_ORDER = 0
DIRECT_MOD = 1000
A_FIRST = 1
GATE_LATE = 0
T_ORDER = (0, 1)
MIX_AT = 7
GADD = 0
GADD_FIRST = 1
TAIL_BUFS = 6
T_FIRST = 0
LATE_GROUPS = 0
LATE_FROM = 0
LATE_EVERY = 3
LATE_PIECES = 1
LATE_1 = ()
LATE_MIX = 1
LATE_OUT = 2
LATE_O = 1
FINISH_LATE = 28

FLOPS = 2 * B * D * U * E * SETS

assert D == P * PACK


def tile_plelayer_pa_kernel(
    tc, x, ews0, ebs0, ew0, eb0, gate_pre0, gb0, sgate_pre, gbs, out_0, out_1
):
    nc = tc.nc
    with ExitStack() as ctx:
        const = ctx.enter_context(tc.tile_pool(name="const", bufs=1))
        raw_pool = ctx.enter_context(tc.tile_pool(name="raw", bufs=RAW_BUFS))
        unit_pool = ctx.enter_context(tc.tile_pool(name="unit", bufs=3))
        held_pool = ctx.enter_context(tc.tile_pool(name="held", bufs=PAIR))
        codes_pool = ctx.enter_context(tc.tile_pool(name="codes", bufs=5))
        h_pool = ctx.enter_context(tc.tile_pool(name="h", bufs=3))
        rows_pool = ctx.enter_context(tc.tile_pool(name="rows", bufs=2))
        part_pool = ctx.enter_context(tc.tile_pool(name="part", bufs=2))
        gated_pool = ctx.enter_context(tc.tile_pool(name="gated", bufs=2))
        tail_pool = ctx.enter_context(tc.tile_pool(name="tail", bufs=TAIL_BUFS))
        psum_mx = ctx.enter_context(tc.psum_pool(name="psum_mx", bufs=2 if SPLIT or HT5 else 3))
        psum_t = ctx.enter_context(tc.psum_pool(name="psum_t", bufs=4))
        psum_acc = ctx.enter_context(tc.psum_pool(name="psum_acc", bufs=1))

        pre_task = const.tile([P, B_BLOCKS, T, G_TASK], BF16)
        for bb in range(B_BLOCKS):
            nc.scalar.dma_start(
                out=pre_task[:, bb],
                in_=gate_pre0[:, bb * P : (bb + 1) * P, :].rearrange("t p g -> p t g"),
            )
        pre_share = const.tile([P, B_BLOCKS, G_SHARE], BF16)
        nc.scalar.dma_start(out=pre_share[:], in_=sgate_pre.rearrange("(bb p) g -> p bb g", p=P))
        gate_row = const.tile([P, T * G_TASK + G_SHARE], BF16)
        nc.gpsimd.memset(gate_row[:], 0.0)
        nc.scalar.dma_start(out=gate_row[0:1, 0 : T * G_TASK], in_=gb0.rearrange("t g -> (t g)").unsqueeze(0))
        nc.scalar.dma_start(out=gate_row[0:1, T * G_TASK :], in_=gbs.unsqueeze(0))
        ones = const.tile([P, P], BF16)
        nc.gpsimd.memset(ones[:], 1.0)
        bias_rows = const.tile([P, P * E], BF16)
        nc.gpsimd.memset(bias_rows[:], 0.0)
        nc.gpsimd.dma_start(out=bias_rows[0:U_BLOCKS, :], in_=ebs0.rearrange("(ub p) e -> ub (p e)", p=P))
        nc.gpsimd.dma_start(
            out=bias_rows[U_BLOCKS : SETS * U_BLOCKS, :], in_=eb0.rearrange("t (ub p) e -> (t ub) (p e)", p=P)
        )
        x_sb = const.tile([P, B_BLOCKS, D], BF16)

        raw_tiles = {}
        code_tiles = {}
        unit_tiles = {}
        readers = {}
        loads = [(s, ub) for s in range(SETS) for ub in range(U_BLOCKS)]
        units = [(s, eg, ub) for s in range(1, 1 + BY_CHUNK) for ub in range(U_BLOCKS) for eg in range(GROUPS)]
        units += [(s, eg, ub) for s in range(1 + BY_CHUNK, SETS) for eg in range(GROUPS) for ub in range(U_BLOCKS)]

        def load_next(pieces=1):
            if loads:
                s, ub = loads.pop(0)
                w = ews0 if s == 0 else ew0[s - 1]
                rows = w.rearrange("(p t) u e -> p t (u e)", t=PACK)
                raw = raw_pool.tile([P, PACK, CHUNK], BF16, name="raw")
                width = CHUNK // pieces
                for piece in range(pieces):
                    nc.sync.dma_start(
                        out=raw[:, :, piece * width : (piece + 1) * width],
                        in_=rows[:, :, ub * CHUNK + piece * width : ub * CHUNK + (piece + 1) * width],
                    )
                raw_tiles[(s, ub)] = raw

        def regroup(unit, engine, first, last, held=False):
            s, eg, ub = unit
            if first == 0:
                pool = held_pool if held else unit_pool
                unit_tiles[unit] = pool.tile([P, E_GROUP, P, PACK], BF16, name="unit", align_bytes=64)
            source = raw_tiles[(s, ub)][:].rearrange("p t (u e) -> p u t e", e=E)
            source = source[:, first:last, :, eg * E_GROUP : (eg + 1) * E_GROUP]
            target = unit_tiles[unit][:].rearrange("p i u t -> p u t i")[:, first:last]
            if engine == "V":
                nc.vector.tensor_copy(out=target, in_=source)
            elif engine == "S":
                nc.scalar.copy(out=target, in_=source)
            else:
                nc.gpsimd.tensor_scalar(
                    out=target, in0=source, scalar1=1.0, scalar2=0.0, op0=ALU.mult, op1=ALU.add
                )
            if last == P:
                readers[(s, ub)] = readers.get((s, ub), 0) + 1
                if readers[(s, ub)] == GROUPS:
                    load_next()

        def quantise(unit):
            s, eg, ub = unit
            if (s, eg) not in code_tiles:
                codes = codes_pool.tile([P, U_BLOCKS * UNIT_WORDS], U32, name="codes", align_bytes=64)
                scales = codes_pool.tile([P, U_BLOCKS * UNIT_WORDS], U8, name="scales", align_bytes=64)
                code_tiles[(s, eg)] = (codes, scales)
            codes, scales = code_tiles[(s, eg)]
            cols = slice(ub * UNIT_WORDS, (ub + 1) * UNIT_WORDS)
            nc.vector.quantize_mx(
                out=codes[:, cols].bitcast(FP8X4),
                scales=scales[:, cols],
                in_=unit_tiles[unit][:].rearrange("p i u t -> p (i u t)"),
            )

        load_next(pieces=2)
        nc.sync.dma_start(out=x_sb[:], in_=x.rearrange("(bb p) d -> p bb d", p=P))
        for count in range(RAW_BUFS - 1):
            load_next()

        g_task = const.tile([P, B_BLOCKS, T * G_TASK], F32)
        g_share = const.tile([P, B_BLOCKS, G_SHARE], F32)

        def softmax_head(logits, rows, width, label):
            wide = [P, rows, width]
            top = const.tile([P, rows], F32, name="top_" + label)
            nc.vector.tensor_reduce(out=top[:], in_=logits, axis=AXIS_X, op=ALU.max)
            nc.vector.tensor_tensor(
                out=logits, in0=logits, in1=top[:].unsqueeze(2).to_broadcast(wide), op=ALU.subtract
            )
            nc.scalar.activation(out=logits, in_=logits, func=ACT.Exp)

        def softmax_tail(logits, rows, width, label):
            wide = [P, rows, width]
            total = const.tile([P, rows], F32, name="total_" + label)
            nc.vector.tensor_reduce(out=total[:], in_=logits, axis=AXIS_X, op=ALU.add)
            inverse = const.tile([P, rows], F32, name="inverse_" + label)
            nc.vector.reciprocal(out=inverse[:], in_=total[:])
            nc.vector.tensor_tensor(
                out=logits, in0=logits, in1=inverse[:].unsqueeze(2).to_broadcast(wide), op=ALU.mult
            )

        gate_bias = psum_t.tile([P, T * G_TASK + G_SHARE], F32, name="h_t")
        nc.tensor.matmul(out=gate_bias[:], lhsT=ones[:], rhs=gate_row[:], start=True, stop=True)
        task_rows = g_task[:].rearrange("p bb (t g) -> p (bb t) g", g=G_TASK)
        nc.vector.tensor_tensor(
            out=g_task[:],
            in0=pre_task[:].rearrange("p bb t g -> p bb (t g)"),
            in1=gate_bias[:, 0 : T * G_TASK].unsqueeze(1).to_broadcast([P, B_BLOCKS, T * G_TASK]),
            op=ALU.add,
        )
        softmax_head(task_rows, B_BLOCKS * T, G_TASK, "task")
        nc.vector.tensor_tensor(
            out=g_share[:],
            in0=pre_share[:],
            in1=gate_bias[:, T * G_TASK :].unsqueeze(1).to_broadcast([P, B_BLOCKS, G_SHARE]),
            op=ALU.add,
        )
        softmax_head(g_share[:], B_BLOCKS, G_SHARE, "share")
        softmax_tail(task_rows, B_BLOCKS * T, G_TASK, "task")
        softmax_tail(g_share[:], B_BLOCKS, G_SHARE, "share")

        ident = const.tile([P, P], F32)
        make_identity(nc, ident[:])
        x_words = x_sb[:].bitcast(F32).rearrange("p bb (w j) -> p bb j w", j=2)
        x_t = psum_t.tile([P, 2, B], F32, name="h_t")
        for bb in range(B_BLOCKS):
            for j in range(2):
                nc.tensor.transpose(
                    out=x_t[:, j, bb * P : (bb + 1) * P], in_=x_words[:, bb, j, :], identity=ident[:]
                )
        x_grouped = const.tile([P, B, PACK], BF16, align_bytes=64)
        nc.scalar.copy(out=x_grouped[:].bitcast(F32), in_=x_t[:].rearrange("p j b -> p b j"))
        x_codes = const.tile([P, B], U32, align_bytes=64)
        x_scales = const.tile([P, B], U8, align_bytes=64)
        nc.vector.quantize_mx(
            out=x_codes[:].bitcast(FP8X4),
            scales=x_scales[:],
            in_=x_grouped[:].rearrange("p b t -> p (b t)"),
        )

        ident_bf = const.tile([P, P], BF16)
        make_identity(nc, ident_bf[:])
        bias_t = psum_t.tile([P, E, P], BF16, name="h_t")
        for e in range(E):
            nc.tensor.transpose(
                out=bias_t[:, e, :],
                in_=bias_rows[:].rearrange("r (p e) -> r e p", e=E)[:, e, :],
                identity=ident_bf[:],
            )
        bias_f = const.tile([P, SETS, U_BLOCKS, E], F32)
        nc.scalar.copy(
            out=bias_f[:].rearrange("p s ub e -> p (s ub) e"),
            in_=bias_t[:, :, 0 : SETS * U_BLOCKS].rearrange("p e r -> p r e"),
        )

        mixer = const.tile([P, N_ROWGROUPS, O_SLOTS, GB], F32)
        nc.gpsimd.memset(mixer[:], 0.0)

        def make_mixer():
            gates_s = const.tile([P, B_BLOCKS, SETS, E], F32)
            nc.vector.tensor_copy(
                out=gates_s[:, :, 0:T, :],
                in_=g_task[:].rearrange("p bb (t g) -> p bb t g", g=G_TASK)[:, :, :, E:G_TASK],
            )
            nc.vector.tensor_copy(out=gates_s[:, :, T, :], in_=g_share[:, :, T * E : G_SHARE])
            own_row = const.tile([P, GB], F32)
            nc.vector.tensor_reduce(
                out=own_row[:], in_=ident[:].rearrange("p (g c) -> p c g", c=GB), axis=AXIS_X, op=ALU.add
            )
            spread = const.tile([P, B_BLOCKS, SETS * E, GB], F32)
            for bb in range(B_BLOCKS):
                nc.vector.tensor_tensor(
                    out=spread[:, bb],
                    in0=gates_s[:, bb].rearrange("p o e -> p (o e)").unsqueeze(2).to_broadcast([P, SETS * E, GB]),
                    in1=own_row[:].unsqueeze(1).to_broadcast([P, SETS * E, GB]),
                    op=ALU.mult,
                )
            per_block = N_ROWGROUPS // B_BLOCKS
            for bb in range(B_BLOCKS):
                turned = psum_t.tile([P, T, P], F32, name="h_t")
                for o in range(T):
                    nc.tensor.transpose(
                        out=turned[:, o, :],
                        in_=spread[:, bb, o * E : (o + 1) * E, :].rearrange("p e c -> p (e c)"),
                        identity=ident[:],
                    )
                nc.scalar.copy(
                    out=mixer[:, bb * per_block : (bb + 1) * per_block, 0:T, :],
                    in_=turned[:].rearrange("p o (g c) -> p g o c", c=GB),
                )
            turned = psum_t.tile([P, B_BLOCKS, P], F32, name="h_t")
            for bb in range(B_BLOCKS):
                nc.tensor.transpose(
                    out=turned[:, bb, :],
                    in_=spread[:, bb, T * E : SETS * E, :].rearrange("p e c -> p (e c)"),
                    identity=ident[:],
                )
            nc.scalar.copy(out=mixer[:, :, T, :], in_=turned[:].rearrange("p bb (g c) -> p (bb g) c", c=GB))

        experts = [(1 + t, e) for t in range(T) for e in range(E)]
        sums = [const.tile([P, B_BLOCKS, U], F32, name="sum_%d" % o) for o in range(SETS)]
        late_part = {(o, 0): const.tile([P, U], F32, name="late_part_%d" % o) for o in range(LATE_O)}
        for o in LATE_1:
            late_part[(o, 1)] = const.tile([P, U], F32, name="late_1_%d" % o)
        tail = const.tile([P, max(GADD, 1)], F32)
        terms = {}
        for o in range(SETS):
            for bb in range(B_BLOCKS):
                terms[(o, bb)] = 0 if (o, bb) in late_part else 1
        hidden_s = [const.tile([P, N_ROWGROUPS, E, GB], F32, name="hidden_s_%d" % ub) for ub in range(U_BLOCKS)]
        products = {}
        hidden = {}
        hidden_t = {}
        gated_tiles = {}
        acc = psum_acc.tile([P, U], F32, name="acc")
        acc2 = []
        last_gated = N_TASK_EXPERTS - 2

        def multiply(s, e):
            eg, i = divmod(e, E_GROUP)
            codes, scales = code_tiles[(s, eg)]
            products[(s, e)] = []
            for half in range(U_BLOCKS // 2):
                if (SPLIT or HT5) and s == 0 and len(products) % 3 == 2 and half == 0:
                    product = psum_acc.tile([P, 2, B], F32, name="spare")
                else:
                    product = psum_mx.tile([P, 2, B], F32, name="product")
                for j in range(2):
                    ub = 2 * half + j
                    cols = slice(ub * UNIT_WORDS + i * P, ub * UNIT_WORDS + (i + 1) * P)
                    nc.tensor.matmul_mx(
                        out=product[:, j, :],
                        lhsT=codes[:, cols].bitcast(FP8X4),
                        lhsT_scale=scales[:, cols],
                        rhs=x_codes[:].bitcast(FP8X4),
                        rhs_scale=x_scales[:],
                        start=True,
                        stop=True,
                    )
                products[(s, e)].append(product)

        def bias_relu(s, e):
            if s > 0:
                hidden[(s, e)] = h_pool.tile([P, U_BLOCKS, B], F32, name="h")
            for ub in range(U_BLOCKS):
                source = products[(s, e)][ub // 2][:, ub % 2, :]
                if s == 0:
                    target = hidden_s[ub][:, :, e, :]
                    source = source.rearrange("p (g c) -> p g c", c=GB)
                else:
                    target = hidden[(s, e)][:, ub, :]
                nc.scalar.activation(
                    out=target, in_=source, func=ACT.Relu, bias=bias_f[:, s, ub, e : e + 1], scale=1.0
                )

        def transpose(n, bb):
            if HT5 and (2 * n + (bb if T_FIRST == 0 else 1 - bb)) % 5 == 4:
                h_t = psum_acc.tile([P, U], F32, name="spare")
            else:
                h_t = psum_t.tile([P, U], F32, name="h_t")
            for ub in range(U_BLOCKS):
                nc.tensor.transpose(
                    out=h_t[:, ub * P : (ub + 1) * P],
                    in_=hidden[experts[n]][:, ub, bb * P : (bb + 1) * P],
                    identity=ident[:],
                )
            hidden_t[(n, bb)] = h_t

        def add_term(o, bb, source, gate, keep=U):
            if terms[(o, bb)] == 0:
                nc.vector.tensor_scalar_mul(out=sums[o][:, bb, 0:keep], in0=source, scalar1=gate)
            else:
                nc.vector.scalar_tensor_tensor(
                    out=sums[o][:, bb, 0:keep], in0=source, scalar=gate, in1=sums[o][:, bb, 0:keep], op0=ALU.mult, op1=ALU.add
                )
            terms[(o, bb)] += 1

        def on_vector(n, bb, which):
            s, e = experts[n]
            col = (s - 1) * G_TASK + e
            if which == 0:
                add_term(s - 1, bb, hidden_t[(n, bb)][:], g_task[:, bb, col : col + 1])
            elif n > last_gated or bb == 1 or n % DIRECT_MOD == DIRECT_MOD - 1:
                col = (s - 1) * E + e
                keep = U if n > last_gated else U - SPLIT * P
                if GADD and bb == 1:
                    keep = U - GADD
                add_term(T, bb, hidden_t[(n, bb)][:, 0:keep], g_share[:, bb, col : col + 1], keep)

        def gate_tail(n):
            s, e = experts[n]
            col = (s - 1) * E + e
            tile = tail_pool.tile([P, GADD], F32, name="gated_g")
            nc.scalar.activation(
                out=tile[:],
                in_=hidden_t[(n, 1)][:, U - GADD : U],
                func=ACT.Copy,
                scale=g_share[:, 1, col : col + 1],
            )
            nc.gpsimd.tensor_tensor(out=tail[:], in0=tile[:], in1=tail[:], op=ALU.add)

        def on_scalar(n):
            s, e = experts[n]
            col = (s - 1) * E + e
            if GADD and GADD_FIRST:
                gate_tail(n)
            if n > last_gated or n % DIRECT_MOD == DIRECT_MOD - 1:
                return
            gated_tiles[n] = gated_pool.tile([P, U], F32, name="gated")
            nc.scalar.activation(
                out=gated_tiles[n][:],
                in_=hidden_t[(n, 0)][:],
                func=ACT.Copy,
                scale=g_share[:, 0, col : col + 1],
            )
            if SPLIT:
                gated_tiles[(n, 1)] = gated_pool.tile([P, SPLIT * P], F32, name="gated_1")
                nc.scalar.activation(
                    out=gated_tiles[(n, 1)][:],
                    in_=hidden_t[(n, 1)][:, U - SPLIT * P : U],
                    func=ACT.Copy,
                    scale=g_share[:, 1, col : col + 1],
                )

        def add_transposed(n):
            for ub in range(U_BLOCKS):
                nc.tensor.matmul(
                    out=acc[:, ub * P : (ub + 1) * P],
                    lhsT=gated_tiles[n][:, ub * P : (ub + 1) * P],
                    rhs=ident[:],
                    start=(n == 0 and ub == 0),
                    stop=(n == last_gated and ub == U_BLOCKS - 1),
                    is_transpose=True,
                )

            if SPLIT:
                if n == 0:
                    acc2.append(psum_acc.tile([P, SPLIT * P], F32, name="spare"))
                for j in range(SPLIT):
                    nc.tensor.matmul(
                        out=acc2[0][:, j * P : (j + 1) * P],
                        lhsT=gated_tiles[(n, 1)][:, j * P : (j + 1) * P],
                        rhs=ident[:],
                        start=(n == 0 and j == 0),
                        stop=(n == last_gated and j == SPLIT - 1),
                        is_transpose=True,
                    )

        def turn_back():
            if SPLIT:
                acc2_sb = gated_pool.tile([P, SPLIT * P], F32, name="gated_1")
                nc.scalar.copy(out=acc2_sb[:], in_=acc2[0][:])
                back2 = psum_t.tile([P, SPLIT * P], F32, name="h_t")
                for j in range(SPLIT):
                    nc.tensor.transpose(
                        out=back2[:, j * P : (j + 1) * P], in_=acc2_sb[:, j * P : (j + 1) * P], identity=ident[:]
                    )
                nc.vector.tensor_tensor(
                    out=sums[T][:, 1, U - SPLIT * P : U], in0=back2[:], in1=sums[T][:, 1, U - SPLIT * P : U], op=ALU.add
                )
            acc_sb = gated_pool.tile([P, U], F32, name="gated")
            nc.scalar.copy(out=acc_sb[:], in_=acc[:])
            back = psum_t.tile([P, U], F32, name="h_t")
            for ub in range(U_BLOCKS):
                nc.tensor.transpose(
                    out=back[:, ub * P : (ub + 1) * P], in_=acc_sb[:, ub * P : (ub + 1) * P], identity=ident[:]
                )
            nc.vector.tensor_tensor(out=sums[T][:, 0, :], in0=back[:], in1=sums[T][:, 0, :], op=ALU.add)

        def finish(o, bb):
            if (o, bb) in late_part:
                nc.vector.tensor_tensor(
                    out=sums[o][:, bb, :], in0=sums[o][:, bb, :], in1=late_part[(o, bb)][:], op=ALU.add
                )
            target = out_0[o] if o < T else out_1
            if GADD and (o, bb) == (T, 1):
                nc.sync.dma_start(out=target[bb * P : (bb + 1) * P, U - GADD : U], in_=tail[:])
                nc.sync.dma_start(out=target[bb * P : (bb + 1) * P, 0 : U - GADD], in_=sums[o][:, bb, 0 : U - GADD])
            else:
                nc.sync.dma_start(out=target[bb * P : (bb + 1) * P, :], in_=sums[o][:, bb, :])

        group_rows = {}
        group_parts = {}
        part_tiles = {}

        def group_turn(g):
            turned_g = psum_t.tile([P, U], F32, name="h_t")
            for ub in range(U_BLOCKS):
                nc.tensor.transpose(
                    out=turned_g[:, ub * P : (ub + 1) * P],
                    in_=hidden_s[ub][:, g].rearrange("p e c -> p (e c)"),
                    identity=ident[:],
                )
            group_rows[g] = rows_pool.tile([P, U], F32, name="rows")
            nc.scalar.copy(out=group_rows[g][:], in_=turned_g[:])

        def group_mix(g, piece=0, pieces=1):
            if piece == 0:
                if PARTS_MX:
                    group_parts[g] = psum_mx.tile([P, U], F32, name="product")
                else:
                    group_parts[g] = psum_t.tile([P, U], F32, name="h_t")
            cols = slice(piece * U // pieces, (piece + 1) * U // pieces)
            nc.tensor.matmul(
                out=group_parts[g][:, cols],
                lhsT=mixer[:, g].rearrange("p o c -> p (o c)"),
                rhs=group_rows[g][:, cols],
                start=True,
                stop=True,
            )

        def group_out(g):
            quad, place = divmod(g, QUAD)
            if place == 0:
                part_tiles[quad] = part_pool.tile([P, QUAD, U], F32, name="part")
            nc.scalar.copy(out=part_tiles[quad][:, place, :], in_=group_parts[g][:])
            if place == QUAD - 1:
                rows = slice(quad * QUAD * GB, (quad + 1) * QUAD * GB)
                for o in range(SETS):
                    target = out_0[o] if o < T else out_1
                    nc.sync.dma_start(
                        out=target[rows, :].rearrange("(q c) u -> c q u", c=GB),
                        in_=part_tiles[quad][o * GB : (o + 1) * GB, :, :],
                    )
            bb, place = divmod(g, N_ROWGROUPS // B_BLOCKS)
            if place == N_ROWGROUPS // B_BLOCKS - 1:
                for o in range(SETS):
                    source = out_0[o] if o < T else out_1
                    target = late_part[(o, bb)][:] if (o, bb) in late_part else sums[o][:, bb, :]
                    nc.sync.dma_start(out=target, in_=source[bb * P : (bb + 1) * P, :])
                    if GADD and (o, bb) == (T, 1):
                        nc.sync.dma_start(out=tail[:], in_=source[bb * P : (bb + 1) * P, U - GADD : U])

        for ub in range(U_BLOCKS):
            pieces = 2 if ub == 0 else 1
            width = P // pieces
            for piece in range(pieces):
                regroup((0, 0, ub), "V", piece * width, (piece + 1) * width)
                regroup((0, 1, ub), SH_ENG[ub], piece * width, (piece + 1) * width)
            if ub > 0:
                quantise((0, 1, ub - 1))
            quantise((0, 0, ub))
        quantise((0, 1, U_BLOCKS - 1))

        def next_unit(k):
            if S_PRE < P and k >= RELU_UNITS:
                regroup(units[k], "V", 0, S_PRE, k == AHEAD - 1)
                regroup(units[k], "S", S_PRE, P)
            else:
                regroup(units[k], "V", 0, P, k == AHEAD - 1)
            if k > 0:
                quantise(units[k - 1])

        if MIX_AT < 0:
            make_mixer()
        if UB_ORDER:
            count = 0
            for ub in range(U_BLOCKS):
                for eg in range(GROUPS):
                    codes, scales = code_tiles[(0, eg)]
                    for pair in range(2):
                        if (SPLIT or HT5) and count % 3 == 2:
                            product = psum_acc.tile([P, 2, B], F32, name="spare")
                        else:
                            product = psum_mx.tile([P, 2, B], F32, name="product")
                        count += 1
                        for j in range(2):
                            i = 2 * pair + j
                            cols = slice(ub * UNIT_WORDS + i * P, ub * UNIT_WORDS + (i + 1) * P)
                            nc.tensor.matmul_mx(
                                out=product[:, j, :],
                                lhsT=codes[:, cols].bitcast(FP8X4),
                                lhsT_scale=scales[:, cols],
                                rhs=x_codes[:].bitcast(FP8X4),
                                rhs_scale=x_scales[:],
                                start=True,
                                stop=True,
                            )
                        for j in range(2):
                            e = eg * E_GROUP + 2 * pair + j
                            nc.scalar.activation(
                                out=hidden_s[ub][:, :, e, :],
                                in_=product[:, j, :].rearrange("p (g c) -> p g c", c=GB),
                                func=ACT.Relu,
                                bias=bias_f[:, 0, ub, e : e + 1],
                                scale=1.0,
                            )
                if ub < RELU_UNITS:
                    next_unit(ub)
                if ub == MIX_AT:
                    make_mixer()
        else:
            for e in range(E):
                multiply(0, e)
                bias_relu(0, e)
                if e < RELU_UNITS:
                    next_unit(e)
                if e == MIX_AT:
                    make_mixer()

        order = list(range(N_ROWGROUPS // 2, N_ROWGROUPS)) + list(range(N_ROWGROUPS // 2))
        rest = AHEAD - RELU_UNITS
        early = order[: N_ROWGROUPS - LATE_GROUPS]
        late = order[N_ROWGROUPS - LATE_GROUPS :]
        group_turn(order[0])
        for j in range(len(early)):
            if j + 1 < len(early):
                group_turn(order[j + 1])
            group_mix(order[j])
            group_out(order[j])
            if j in LEAD_AT:
                n = LEAD_AT.index(j)
                multiply(*experts[n])
                bias_relu(*experts[n])
            for k in range(j * rest // len(early), (j + 1) * rest // len(early)):
                next_unit(RELU_UNITS + k)
        quantise(units[AHEAD - 1])

        g_units = len(units) - AHEAD
        if PAIR > 1:
            batches = [list(range(k, min(k + PAIR, len(units)))) for k in range(AHEAD, len(units), PAIR)]
        else:
            batches = [[k] for k in range(AHEAD, len(units))]
        g_batches = len(batches)
        quant_steps = [Q_FIRST + (Q_LAST - Q_FIRST) * j // (g_batches - 1) for j in range(g_batches)]
        ctx.enter_context(tc.manual_schedule())
        todo = []
        qpos = quant_steps if QSTEP == 0 else [Q_FIRST * 3 + QSTEP * j for j in range(g_batches)]
        if QSTEP == 0:
            qpos = [3 * q for q in quant_steps]

        def slot(place):
            if place in qpos:
                j = qpos.index(place)
                for k in batches[j]:
                    quantise(units[k])
                if j + 1 < g_batches:
                    for k in batches[j + 1]:
                        regroup(units[k], "G", 0, G_CUT, True)
                    todo.extend(batches[j + 1])

        for i in range(FIRST_I, N_TASK_EXPERTS + ADD_LAG + 1):
            if i == FIRST_I:
                for k in batches[0]:
                    regroup(units[k], "G", 0, G_CUT, True)
                todo += batches[0]
            slot(3 * i)
            if 2 <= i < N_TASK_EXPERTS + 2:
                if (i - 2 <= last_gated or GADD) and not GATE_LATE:
                    on_scalar(i - 2)
                on_vector(i - 2, 1, 0)
                slot(3 * i + 1)
                on_vector(i - 2, 1, 1)
                slot(3 * i + 2)
                on_vector(i - 2, 0, 0)
                on_vector(i - 2, 0, 1)
            else:
                slot(3 * i + 1)
                slot(3 * i + 2)
            if len(LEAD_AT) <= i < N_TASK_EXPERTS:
                multiply(*experts[i])
                bias_relu(*experts[i])
            if GATE_LATE and 2 <= i <= last_gated + 2:
                on_scalar(i - 2)
            if todo and G_CUT < P:
                regroup(units[todo.pop(0)], "S", G_CUT, P)
            if A_FIRST and ADD_LAG <= i <= last_gated + ADD_LAG:
                add_transposed(i - ADD_LAG)
            for bb in T_ORDER:
                if 1 <= i <= N_TASK_EXPERTS:
                    transpose(i - 1, bb)
                if late and LATE_PIECES == 4 and i >= LATE_FROM:
                    j, place = divmod(i - LATE_FROM, LATE_EVERY)
                    if place in (LATE_MIX, LATE_MIX + 1) and j < len(late):
                        group_mix(late[j], 2 * (place - LATE_MIX) + bb, 4)
            if not A_FIRST and ADD_LAG <= i <= last_gated + ADD_LAG and (i - ADD_LAG) % DIRECT_MOD != DIRECT_MOD - 1:
                add_transposed(i - ADD_LAG)
            if late and i >= LATE_FROM:
                j, place = divmod(i - LATE_FROM, LATE_EVERY)
                if place == 0 and j < len(late):
                    group_turn(late[j])
                if LATE_PIECES == 1 and place == LATE_MIX and j < len(late):
                    group_mix(late[j])
                if LATE_PIECES == 2 and place in (LATE_MIX, LATE_MIX + 1) and j < len(late):
                    group_mix(late[j], place - LATE_MIX, 2)
                jj = j - LATE_OUT // LATE_EVERY
                if place == LATE_OUT % LATE_EVERY and 0 <= jj < len(late):
                    group_out(late[jj])
            if i == last_gated + ADD_LAG:
                turn_back()
            if i >= 2 and (i - 2) % E == E - 1:
                o = (i - 2) // E
                if i < N_TASK_EXPERTS + 1:
                    finish(o, 1)
                else:
                    finish(o, 1)
                if not late or (o, 0) not in late_part or i >= FINISH_LATE:
                    finish(o, 0)
            if late and i == FINISH_LATE:
                for o in range(LATE_O):
                    if o * E + E - 1 + 2 < FINISH_LATE:
                        finish(o, 0)
        for bb in range(B_BLOCKS):
            finish(T, bb)
